import numpy as np
import ml_dtypes


def mxq(x, axis, fmt="e4m3"):
    dtype, down = {"e4m3": (ml_dtypes.float8_e4m3fn, 7), "e5m2": (ml_dtypes.float8_e5m2, 14)}[fmt]
    v = np.moveaxis(np.asarray(x, np.float32).astype(ml_dtypes.bfloat16).astype(np.float64), axis, -1)
    blocks = v.reshape(v.shape[:-1] + (-1, 32))
    amax = np.abs(blocks).max(-1, keepdims=True)
    byte = np.maximum(np.where(amax > 0, np.frexp(amax)[1] - 1 + 127, 0) - down, 1)
    scale = np.exp2(byte - 127.0)
    codes = (blocks / scale).astype(np.float32).astype(dtype).astype(np.float64)
    return np.moveaxis((codes * scale).reshape(v.shape), -1, axis)


WIDE = False


def mx_kscale(k):
    if not WIDE:
        return np.ones(k)
    levels = np.array([10, -10, 5, -5, 0])
    if k % 512:
        return np.exp2(np.random.permutation(np.resize(levels, k // 32))).repeat(32)
    a = np.empty((k // 512, 16))
    for p in range(k // 512):
        a[p, :8] = np.random.permutation(np.resize(levels, 8))
        for g in range(8):
            far = levels[np.abs(levels - a[p, g]) >= 10]
            a[p, g + 8] = far[np.random.randint(len(far))]
    return np.exp2(a.ravel()).repeat(32)


BF16 = ml_dtypes.bfloat16


def bf(x):
    return np.asarray(x, np.float32).astype(BF16)


def f64(x):
    return np.asarray(x).astype(np.float64)


E2M1 = np.array([0.0, 0.5, 1.0, 1.5, 2.0, 3.0, 4.0, 6.0, -0.0, -0.5, -1.0, -1.5, -2.0, -3.0, -4.0, -6.0])


def pack_weight(w, fmt):
    k, n = w.shape
    w = f64(bf(w)).reshape(k // 32, 32, n)
    amax = np.abs(w).max(1)
    if fmt == "e4m3":
        byte = np.frexp(amax)[1] - 1 + 127 - 7
    else:
        mant, ex = np.frexp(amax / 6.0)
        byte = np.where(mant > 0.5, ex, ex - 1) + 127
    byte = np.clip(np.where(amax > 0, byte, 1), 1, 254)
    scaled = (w * np.exp2(127.0 - byte)[:, None, :]).reshape(k, n).astype(np.float32)
    by_word = np.ascontiguousarray(scaled.reshape(k // 512, 128, 4, n).transpose(0, 1, 3, 2))
    if fmt == "e4m3":
        words = by_word.astype(ml_dtypes.float8_e4m3fn).view(np.uint8)
    else:
        c = by_word.astype(ml_dtypes.float4_e2m1fn).view(np.uint8) & 0xF
        words = c[..., 0::2] | (c[..., 1::2] << 4)
    return np.ascontiguousarray(words), np.ascontiguousarray(byte.astype(np.uint8).reshape(k // 512, 16, n))


def unpack_weight(words, scales, fmt):
    g, p, n, _ = words.shape
    if fmt == "e4m3":
        vals = np.ascontiguousarray(words).view(ml_dtypes.float8_e4m3fn).astype(np.float64)
    else:
        nib = np.empty((g, p, n, 4), np.uint8)
        nib[..., 0::2] = words & 0xF
        nib[..., 1::2] = words >> 4
        vals = E2M1[nib]
    vals = vals * np.repeat(np.exp2(scales.astype(np.float64) - 127.0), 8, axis=1)[..., None]
    return vals.transpose(0, 1, 3, 2).reshape(g * 512, n)


E, F, H, MID, OUT = 16384, 64, 192, 512, 128
D = 2 * (F + H)
IN = D + 1
FMT = "e4m3"


def setup_inputs():
    s = mx_kscale(D)
    t = mx_kscale(MID)
    w1 = np.concatenate([np.random.standard_normal((MID, D)) / np.sqrt(D) / s[None, :],
                         np.random.standard_normal((MID, 1)) * 0.5], axis=1) * t[:, None]
    dst_node_feat = bf(np.random.standard_normal((E, F)) * s[:F])
    dst_node_hidden = bf(np.random.standard_normal((E, H)) * s[F:F + H])
    src_node_feat = bf(np.random.standard_normal((E, F)) * s[F + H:2 * F + H])
    src_node_hidden = bf(np.random.standard_normal((E, H)) * s[2 * F + H:])
    edge_feat = bf(np.random.standard_normal(E))
    b1 = bf(np.random.standard_normal(MID) * 0.3 * t)
    w2 = np.random.standard_normal((OUT, MID)) / np.sqrt(MID) / t[None, :]
    w2_words, w2_scales = pack_weight(np.ascontiguousarray(w2.T), FMT)
    b2 = bf(np.random.standard_normal(OUT) * 0.3)
    return {"dst_node_feat": dst_node_feat,
            "dst_node_hidden": dst_node_hidden,
            "src_node_feat": src_node_feat,
            "src_node_hidden": src_node_hidden,
            "edge_feat": edge_feat,
            "W1": bf(w1),
            "b1": b1,
            "W2_words": w2_words,
            "W2_scales": w2_scales,
            "b2": b2}


def reference(dst_node_feat, dst_node_hidden, src_node_feat, src_node_hidden, edge_feat, W1, b1, W2_words, W2_scales, b2):
    x = np.concatenate([f64(dst_node_feat), f64(dst_node_hidden), f64(src_node_feat), f64(src_node_hidden),
                        f64(edge_feat)[:, None]], axis=1)
    w1 = f64(W1)
    pre = (mxq(x[:, :D], 1, "e4m3") @ mxq(w1[:, :D], 1, "e4m3").T) + x[:, D:] * w1[:, D] + f64(b1)
    h = np.maximum(pre, 0.0)
    return np.tanh((mxq(h, 1, "e4m3") @ unpack_weight(W2_words, W2_scales, FMT)) + f64(b2))

@@ -1,0 +1,341 @@
+from contextlib import ExitStack
+
+import concourse.mybir as mybir
+from concourse.masks import make_identity
+
+F32 = mybir.dt.float32
+BF16 = mybir.dt.bfloat16
+U32 = mybir.dt.uint32
+U8 = mybir.dt.uint8
+I32 = mybir.dt.int32
+FP8X4 = mybir.dt.float8_e4m3fn_x4
+ALU = mybir.AluOpType
+ACT = mybir.ActivationFunctionType
+
+P = 128
+PACK = 4
+E, F, H, MID, OUT = 16384, 64, 192, 512, 128
+NODE = 2 * (F + H)
+NODE_WORDS = NODE // 2
+
+TILES_PER_GROUP = 4
+TILES_PER_CHUNK = 8
+GROUPS_PER_CHUNK = TILES_PER_CHUNK // TILES_PER_GROUP
+N_CHUNKS = E // (P * TILES_PER_CHUNK)
+N_GROUPS = N_CHUNKS * GROUPS_PER_CHUNK
+CHUNKS_AHEAD = 3
+EDGE_TERM_AHEAD = 5
+
+N_TILES = N_GROUPS * TILES_PER_GROUP
+SUMS1_BANKS = 3
+RUN = 4
+
+FLOPS = 2 * E * ((NODE + 1) * MID + MID * OUT)
+
+
+def tile_edgenetwork_kernel(
+    tc,
+    dst_node_feat,
+    dst_node_hidden,
+    src_node_feat,
+    src_node_hidden,
+    edge_feat,
+    W1,
+    b1,
+    W2_words,
+    W2_scales,
+    b2,
+    out,
+):
+    nc = tc.nc
+
+    def by_chunk(rows):
+        return rows.rearrange("(q c i) f -> q c i f", c=P, i=TILES_PER_CHUNK)
+
+    node_inputs = (
+        (by_chunk(dst_node_feat), 0, 0, F),
+        (by_chunk(dst_node_hidden), 0, F, 2 * F),
+        (by_chunk(dst_node_hidden), 2 * F, 3 * F, F),
+        (by_chunk(src_node_feat), 0, F + H, F),
+        (by_chunk(src_node_hidden), 0, 2 * F + H, 2 * F),
+        (by_chunk(src_node_hidden), 2 * F, 4 * F + H, F),
+    )
+    out_by_chunk = by_chunk(out)
+
+    with ExitStack() as stack:
+        const = stack.enter_context(tc.tile_pool(name="const", bufs=1))
+        work = stack.enter_context(tc.tile_pool(name="work", bufs=2))
+        psum = stack.enter_context(tc.psum_pool(name="psum", bufs=1))
+        stack.enter_context(tc.manual_schedule())
+
+        x_chunks = {}
+
+        def load_chunk(q):
+            x_sb = work.tile([P, TILES_PER_CHUNK, NODE], BF16, tag="x", bufs=CHUNKS_AHEAD + 1, name="x_sb")
+            for rows, first_in, first_x, width in node_inputs:
+                nc.sync.dma_start(
+                    out=x_sb[:, :, first_x : first_x + width], in_=rows[q][:, :, first_in : first_in + width]
+                )
+            x_chunks[q] = x_sb
+
+        w1_rows = const.tile([P, PACK, NODE + 1], BF16)
+        nc.sync.dma_start(out=w1_rows[:], in_=W1.rearrange("(j t) k -> j t k", t=PACK))
+        load_chunk(0)
+        edge_cols = const.tile([P, N_CHUNKS * TILES_PER_CHUNK], BF16)
+        nc.scalar.dma_start(
+            out=edge_cols[:].rearrange("c (q i) -> c q i", i=TILES_PER_CHUNK),
+            in_=edge_feat.rearrange("(q c i) -> c q i", c=P, i=TILES_PER_CHUNK),
+        )
+        b1_bf = const.tile([P, PACK], BF16)
+        nc.scalar.dma_start(out=b1_bf[:], in_=b1.rearrange("(p t) -> p t", t=PACK))
+        b2_bf = const.tile([P, 1], BF16)
+        nc.scalar.dma_start(out=b2_bf[:], in_=b2.rearrange("(p o) -> p o", o=1))
+        load_chunk(1)
+
+        w2_codes = const.tile([P, OUT * PACK], U8, align_bytes=64)
+        nc.sync.dma_start(
+            out=w2_codes[:].bitcast(I32),
+            in_=W2_words.rearrange("g p n t -> (g p) (n t)").bitcast(I32),
+        )
+        w2_scales = const.tile([P, OUT], U8, align_bytes=64)
+        nc.vector.memset(w2_scales[:].bitcast(I32), 0)
+        for quadrant in range(4):
+            nc.sync.dma_start(
+                out=w2_scales[32 * quadrant : 32 * quadrant + 4, :].bitcast(I32),
+                in_=W2_scales[0, 4 * quadrant : 4 * quadrant + 4, :].bitcast(I32),
+            )
+        load_chunk(2)
+
+        ident_f32 = const.tile([P, P], F32)
+        make_identity(nc, ident_f32[:])
+        ident_bf = const.tile([P, P], BF16)
+        make_identity(nc, ident_bf[:])
+
+        w1_nodes = const.tile([P, PACK, NODE], BF16)
+        nc.vector.tensor_copy(out=w1_nodes[:], in_=w1_rows[:, :, 0:NODE])
+        w1_edge = const.tile([P, PACK], F32)
+        nc.vector.tensor_copy(out=w1_edge[:], in_=w1_rows[:, :, NODE])
+        b1_f32 = const.tile([P, PACK], F32)
+        nc.vector.tensor_copy(out=b1_f32[:], in_=b1_bf[:])
+        b2_f32 = const.tile([P, 1], F32)
+        nc.vector.tensor_copy(out=b2_f32[:], in_=b2_bf[:])
+
+        def transpose_rows(row_tiles):
+            banks = []
+            for pair in range(2):
+                xt = psum.tile([P, 4, P], F32, tag="xt", bufs=2, name="xt")
+                for i in range(2):
+                    words = row_tiles[2 * pair + i].bitcast(F32)
+                    for u in range(2):
+                        nc.tensor.transpose(xt[:, 2 * i + u, :], words[:, u:NODE_WORDS:2], ident_f32[:])
+                banks.append(xt)
+            return banks
+
+        def new_grouped():
+            return work.tile([P, TILES_PER_GROUP * P * PACK], BF16, tag="grouped", align_bytes=64, name="grouped")
+
+        def copy_out(banks, grouped, pair):
+            grouped_words = grouped[:].bitcast(F32)
+            nc.scalar.copy(
+                out=grouped_words[:, 512 * pair : 512 * (pair + 1)].rearrange("p (i c u) -> p i c u", i=2, u=2),
+                in_=banks[pair][:].rearrange("p (i u) c -> p i c u", u=2),
+            )
+
+        def quantise(grouped, codes, scales):
+            nc.vector.quantize_mx(out=codes.bitcast(FP8X4), scales=scales, in_=grouped)
+
+        w1_codes = const.tile([P, PACK * P], U32, align_bytes=64)
+        w1_scales = const.tile([P, PACK * P], U8, align_bytes=64)
+        w1_banks = transpose_rows([w1_nodes[:, t, :] for t in range(PACK)])
+        w1_grouped = new_grouped()
+        copy_out(w1_banks, w1_grouped, 0)
+        copy_out(w1_banks, w1_grouped, 1)
+        quantise(w1_grouped[:], w1_codes[:], w1_scales[:])
+
+        def in_range(g):
+            return 0 <= g < N_GROUPS
+
+        edge_terms = {}
+
+        spreads = {}
+
+        def spread_edge(g):
+            if not in_range(g):
+                return
+            q, half = divmod(g, GROUPS_PER_CHUNK)
+            if half == 0:
+                spreads[q] = psum.tile([P, TILES_PER_CHUNK, P], BF16, tag="spread", name="spread")
+            for j in range(TILES_PER_GROUP):
+                i = TILES_PER_GROUP * half + j
+                m = TILES_PER_CHUNK * q + i
+                nc.tensor.matmul(
+                    out=spreads[q][:, i, :],
+                    lhsT=edge_cols[:, m : m + 1].to_broadcast([P, P]),
+                    rhs=ident_bf[:],
+                    start=True,
+                    stop=True,
+                )
+
+        def prepare_edge_term(g):
+            if not in_range(g) or g % GROUPS_PER_CHUNK != GROUPS_PER_CHUNK - 1:
+                return
+            q = g // GROUPS_PER_CHUNK
+            edge_all = work.tile([P, TILES_PER_CHUNK, P], BF16, tag="edge_all", name="edge_all")
+            nc.vector.tensor_copy(out=edge_all[:], in_=spreads[q][:])
+            edge_term = work.tile([P, PACK, TILES_PER_CHUNK, P], F32, tag="edge_term", bufs=3, name="edge_term")
+            for t in range(PACK):
+                nc.gpsimd.tensor_scalar(
+                    out=edge_term[:, t, :, :],
+                    in0=edge_all[:],
+                    scalar1=w1_edge[:, t : t + 1],
+                    scalar2=b1_f32[:, t : t + 1],
+                    op0=ALU.mult,
+                    op1=ALU.add,
+                )
+            edge_terms[q] = edge_term
+
+        x_grouped = {}
+        x_codes = {}
+        x_scales = {}
+        sums1 = {}
+        h_grouped = {}
+        h_codes = {}
+        h_scales = {}
+        sums2 = {}
+
+        x_banks = {}
+
+        def transpose_x(g):
+            if not in_range(g):
+                return
+            q, half = divmod(g, GROUPS_PER_CHUNK)
+            if half == 0 and q + CHUNKS_AHEAD < N_CHUNKS:
+                load_chunk(q + CHUNKS_AHEAD)
+            x_sb = x_chunks[q]
+            x_banks[g] = transpose_rows([x_sb[:, TILES_PER_GROUP * half + j, :] for j in range(TILES_PER_GROUP)])
+
+        def copy_out_x(g, pair):
+            if not in_range(g):
+                return
+            if pair == 0:
+                x_grouped[g] = new_grouped()
+            copy_out(x_banks[g], x_grouped[g], pair)
+
+        def quantise_x(g):
+            if not in_range(g):
+                return
+            x_codes[g] = work.tile([P, TILES_PER_GROUP * P], U32, tag="x_codes", align_bytes=64, name="x_codes")
+            x_scales[g] = work.tile([P, TILES_PER_GROUP * P], U8, tag="x_scales", align_bytes=64, name="x_scales")
+            quantise(x_grouped[g][:], x_codes[g][:], x_scales[g][:])
+
+        def layer1(n):
+            if not 0 <= n < N_TILES:
+                return
+            g, j = divmod(n, TILES_PER_GROUP)
+            sums = psum.tile([P, PACK, P], F32, tag="sums1", bufs=SUMS1_BANKS, name="sums1_tile")
+            cols = slice(P * j, P * (j + 1))
+            for t in range(PACK):
+                block = slice(P * t, P * (t + 1))
+                nc.tensor.matmul_mx(
+                    out=sums[:, t, :],
+                    lhsT=w1_codes[:, block].bitcast(FP8X4),
+                    lhsT_scale=w1_scales[:, block],
+                    rhs=x_codes[g][:, cols].bitcast(FP8X4),
+                    rhs_scale=x_scales[g][:, cols],
+                    start=True,
+                    stop=True,
+                )
+            sums1[n] = sums
+
+        def hidden(n):
+            if not 0 <= n < N_TILES:
+                return
+            g, j = divmod(n, TILES_PER_GROUP)
+            q, i = divmod(n, TILES_PER_CHUNK)
+            if j == 0:
+                h_grouped[g] = work.tile([P, TILES_PER_GROUP, P * PACK], BF16, tag="h", bufs=3, align_bytes=64, name="h")
+            pre = work.tile([P, PACK, P], BF16, tag="pre", bufs=3, name="pre")
+            nc.vector.tensor_tensor(
+                out=pre[:],
+                in0=sums1[n][:],
+                in1=edge_terms[q][:, :, i, :],
+                op=ALU.add,
+            )
+            nc.scalar.activation(
+                out=h_grouped[g][:, j, :].rearrange("p (b i t) -> p b t i", i=RUN, t=PACK),
+                in_=pre[:].rearrange("p t (b i) -> p b t i", i=RUN),
+                func=ACT.Relu,
+            )
+
+        def quantise_h(g):
+            if not in_range(g):
+                return
+            h_codes[g] = work.tile([P, TILES_PER_GROUP * P], U32, tag="h_codes", align_bytes=64, name="h_codes")
+            h_scales[g] = work.tile([P, TILES_PER_GROUP * P], U8, tag="h_scales", align_bytes=64, name="h_scales")
+            quantise(h_grouped[g][:].rearrange("p j w -> p (j w)"), h_codes[g][:], h_scales[g][:])
+
+        def layer2(g):
+            if not in_range(g):
+                return
+            sums = psum.tile([P, TILES_PER_GROUP * P], F32, tag="sums2", name="sums2_tile")
+            nc.tensor.matmul_mx(
+                out=sums[:],
+                lhsT=w2_codes[:].bitcast(FP8X4),
+                lhsT_scale=w2_scales[:],
+                rhs=h_codes[g][:].bitcast(FP8X4),
+                rhs_scale=h_scales[g][:],
+                start=True,
+                stop=True,
+            )
+            sums2[g] = sums
+
+        out_rows = {}
+        out_banks = {}
+
+        def tanh(g):
+            if not in_range(g):
+                return
+            out_rows[g] = work.tile([P, TILES_PER_GROUP * P], F32, tag="out_rows", name="out_rows")
+            nc.scalar.activation(out=out_rows[g][:], in_=sums2[g][:], func=ACT.Tanh, bias=b2_f32[:, 0:1])
+
+        def transpose_out(g):
+            if not in_range(g):
+                return
+            bank = psum.tile([P, TILES_PER_GROUP, OUT], F32, tag="out_bank", name="out_bank")
+            for j in range(TILES_PER_GROUP):
+                nc.tensor.transpose(bank[:, j, :], out_rows[g][:, P * j : P * (j + 1)], ident_f32[:])
+            out_banks[g] = bank
+
+        def store(g):
+            if not in_range(g):
+                return
+            q, half = divmod(g, GROUPS_PER_CHUNK)
+            result = work.tile([P, TILES_PER_GROUP, OUT], F32, tag="result", bufs=3, name="result")
+            nc.scalar.copy(out=result[:], in_=out_banks[g][:])
+            first = TILES_PER_GROUP * half
+            nc.sync.dma_start(out=out_by_chunk[q][:, first : first + TILES_PER_GROUP, :], in_=result[:])
+
+        for g in range(-2 - EDGE_TERM_AHEAD, -2):
+            spread_edge(g + EDGE_TERM_AHEAD)
+            prepare_edge_term(g + EDGE_TERM_AHEAD)
+        for g in range(-2, N_GROUPS + 2):
+            first_tile = TILES_PER_GROUP * g
+            transpose_x(g + 2)
+            spread_edge(g + EDGE_TERM_AHEAD)
+            hidden(first_tile)
+            layer1(first_tile + SUMS1_BANKS)
+            copy_out_x(g + 2, 0)
+            quantise_x(g + 1)
+            hidden(first_tile + 1)
+            layer1(first_tile + 1 + SUMS1_BANKS)
+            copy_out_x(g + 2, 1)
+            prepare_edge_term(g + EDGE_TERM_AHEAD)
+            transpose_out(g - 2)
+            hidden(first_tile + 2)
+            layer1(first_tile + 2 + SUMS1_BANKS)
+            store(g - 2)
+            quantise_h(g - 1)
+            layer2(g - 1)
+            hidden(first_tile + 3)
+            layer1(first_tile + 3 + SUMS1_BANKS)
+            tanh(g - 1)

@@ -29,6 +29,7 @@ EDGE_TERM_AHEAD = 5
 N_TILES = N_GROUPS * TILES_PER_GROUP
 SUMS1_BANKS = 3
 RUN = 4
+RELU_ON_VECTOR = 1
 
 FLOPS = 2 * E * ((NODE + 1) * MID + MID * OUT)
 
@@ -247,25 +248,31 @@ def tile_edgenetwork_kernel(
                 )
             sums1[n] = sums
 
+        pre_grouped = {}
+
         def hidden(n):
             if not 0 <= n < N_TILES:
                 return
             g, j = divmod(n, TILES_PER_GROUP)
             q, i = divmod(n, TILES_PER_CHUNK)
             if j == 0:
+                pre_grouped[g] = work.tile([P, TILES_PER_GROUP, P * PACK], BF16, tag="pre", bufs=3, align_bytes=64, name="pre")
                 h_grouped[g] = work.tile([P, TILES_PER_GROUP, P * PACK], BF16, tag="h", bufs=3, align_bytes=64, name="h")
-            pre = work.tile([P, PACK, P], BF16, tag="pre", bufs=3, name="pre")
             nc.vector.tensor_tensor(
-                out=pre[:],
-                in0=sums1[n][:],
-                in1=edge_terms[q][:, :, i, :],
+                out=pre_grouped[g][:, j, :].rearrange("p (b i t) -> p b t i", i=RUN, t=PACK),
+                in0=sums1[n][:].rearrange("p t (b i) -> p b t i", i=RUN),
+                in1=edge_terms[q][:, :, i, :].rearrange("p t (b i) -> p b t i", i=RUN),
                 op=ALU.add,
             )
-            nc.scalar.activation(
-                out=h_grouped[g][:, j, :].rearrange("p (b i t) -> p b t i", i=RUN, t=PACK),
-                in_=pre[:].rearrange("p t (b i) -> p b t i", i=RUN),
-                func=ACT.Relu,
-            )
+
+        def relu(n):
+            if not 0 <= n < N_TILES:
+                return
+            g, j = divmod(n, TILES_PER_GROUP)
+            if j < RELU_ON_VECTOR:
+                nc.vector.tensor_scalar_max(out=h_grouped[g][:, j, :], in0=pre_grouped[g][:, j, :], scalar1=0.0)
+            else:
+                nc.scalar.activation(out=h_grouped[g][:, j, :], in_=pre_grouped[g][:, j, :], func=ACT.Relu)
 
         def quantise_h(g):
             if not in_range(g):
@@ -328,14 +335,18 @@ def tile_edgenetwork_kernel(
             quantise_x(g + 1)
             hidden(first_tile + 1)
             layer1(first_tile + 1 + SUMS1_BANKS)
+            relu(first_tile)
+            relu(first_tile + 1)
             copy_out_x(g + 2, 1)
             prepare_edge_term(g + EDGE_TERM_AHEAD)
             transpose_out(g - 2)
             hidden(first_tile + 2)
             layer1(first_tile + 2 + SUMS1_BANKS)
+            relu(first_tile + 2)
             store(g - 2)
             quantise_h(g - 1)
             layer2(g - 1)
             hidden(first_tile + 3)
             layer1(first_tile + 3 + SUMS1_BANKS)
+            relu(first_tile + 3)
             tanh(g - 1)

@@ -24,12 +24,10 @@ GROUPS_PER_CHUNK = TILES_PER_CHUNK // TILES_PER_GROUP
 N_CHUNKS = E // (P * TILES_PER_CHUNK)
 N_GROUPS = N_CHUNKS * GROUPS_PER_CHUNK
 CHUNKS_AHEAD = 3
-EDGE_TERM_AHEAD = 5
-
-N_TILES = N_GROUPS * TILES_PER_GROUP
-SUMS1_BANKS = 3
 RUN = 4
 RELU_ON_VECTOR = 1
+GROUP_VALUES = TILES_PER_GROUP * P * PACK
+GROUP_WORDS = TILES_PER_GROUP * P
 
 FLOPS = 2 * E * ((NODE + 1) * MID + MID * OUT)
 
@@ -51,7 +49,7 @@ def tile_edgenetwork_kernel(
     nc = tc.nc
 
     def by_chunk(rows):
-        return rows.rearrange("(q c i) f -> q c i f", c=P, i=TILES_PER_CHUNK)
+        return rows.rearrange("(q i c) f -> q c i f", c=P, i=TILES_PER_CHUNK)
 
     node_inputs = (
         (by_chunk(dst_node_feat), 0, 0, F),
@@ -62,6 +60,7 @@ def tile_edgenetwork_kernel(
         (by_chunk(src_node_hidden), 2 * F, 4 * F + H, F),
     )
     out_by_chunk = by_chunk(out)
+    edge_by_chunk = edge_feat.rearrange("(q e) -> q e", e=P * TILES_PER_CHUNK)
 
     with ExitStack() as stack:
         const = stack.enter_context(tc.tile_pool(name="const", bufs=1))
@@ -70,8 +69,11 @@ def tile_edgenetwork_kernel(
         stack.enter_context(tc.manual_schedule())
 
         x_chunks = {}
+        edge_all = {}
 
         def load_chunk(q):
+            edge_all[q] = work.tile([P, P * TILES_PER_CHUNK], BF16, tag="edge_all", bufs=CHUNKS_AHEAD + 2, name="edge_all")
+            nc.sync.dma_start(out=edge_all[q][:], in_=edge_by_chunk[q].partition_broadcast(P))
             x_sb = work.tile([P, TILES_PER_CHUNK, NODE], BF16, tag="x", bufs=CHUNKS_AHEAD + 1, name="x_sb")
             for rows, first_in, first_x, width in node_inputs:
                 nc.sync.dma_start(
@@ -81,16 +83,11 @@ def tile_edgenetwork_kernel(
 
         w1_rows = const.tile([P, PACK, NODE + 1], BF16)
         nc.sync.dma_start(out=w1_rows[:], in_=W1.rearrange("(j t) k -> j t k", t=PACK))
-        load_chunk(0)
-        edge_cols = const.tile([P, N_CHUNKS * TILES_PER_CHUNK], BF16)
-        nc.scalar.dma_start(
-            out=edge_cols[:].rearrange("c (q i) -> c q i", i=TILES_PER_CHUNK),
-            in_=edge_feat.rearrange("(q c i) -> c q i", c=P, i=TILES_PER_CHUNK),
-        )
         b1_bf = const.tile([P, PACK], BF16)
         nc.scalar.dma_start(out=b1_bf[:], in_=b1.rearrange("(p t) -> p t", t=PACK))
         b2_bf = const.tile([P, 1], BF16)
         nc.scalar.dma_start(out=b2_bf[:], in_=b2.rearrange("(p o) -> p o", o=1))
+        load_chunk(0)
         load_chunk(1)
 
         w2_codes = const.tile([P, OUT * PACK], U8, align_bytes=64)
@@ -109,8 +106,6 @@ def tile_edgenetwork_kernel(
 
         ident_f32 = const.tile([P, P], F32)
         make_identity(nc, ident_f32[:])
-        ident_bf = const.tile([P, P], BF16)
-        make_identity(nc, ident_bf[:])
 
         w1_nodes = const.tile([P, PACK, NODE], BF16)
         nc.vector.tensor_copy(out=w1_nodes[:], in_=w1_rows[:, :, 0:NODE])
@@ -132,78 +127,50 @@ def tile_edgenetwork_kernel(
                 banks.append(xt)
             return banks
 
-        def new_grouped():
-            return work.tile([P, TILES_PER_GROUP * P * PACK], BF16, tag="grouped", align_bytes=64, name="grouped")
-
         def copy_out(banks, grouped, pair):
-            grouped_words = grouped[:].bitcast(F32)
+            grouped_words = grouped.bitcast(F32)
             nc.scalar.copy(
                 out=grouped_words[:, 512 * pair : 512 * (pair + 1)].rearrange("p (i c u) -> p i c u", i=2, u=2),
                 in_=banks[pair][:].rearrange("p (i u) c -> p i c u", u=2),
             )
 
-        def quantise(grouped, codes, scales):
-            nc.vector.quantize_mx(out=codes.bitcast(FP8X4), scales=scales, in_=grouped)
-
         w1_codes = const.tile([P, PACK * P], U32, align_bytes=64)
         w1_scales = const.tile([P, PACK * P], U8, align_bytes=64)
         w1_banks = transpose_rows([w1_nodes[:, t, :] for t in range(PACK)])
-        w1_grouped = new_grouped()
-        copy_out(w1_banks, w1_grouped, 0)
-        copy_out(w1_banks, w1_grouped, 1)
-        quantise(w1_grouped[:], w1_codes[:], w1_scales[:])
+        w1_grouped = const.tile([P, GROUP_VALUES], BF16, align_bytes=64)
+        copy_out(w1_banks, w1_grouped[:], 0)
+        copy_out(w1_banks, w1_grouped[:], 1)
+        nc.vector.quantize_mx(out=w1_codes[:].bitcast(FP8X4), scales=w1_scales[:], in_=w1_grouped[:])
 
         def in_range(g):
             return 0 <= g < N_GROUPS
 
+        to_quantise = {}
         edge_terms = {}
 
-        spreads = {}
+        def new_to_quantise(k):
+            to_quantise[k] = work.tile([P, 2 * GROUP_VALUES], BF16, tag="ring", bufs=3, align_bytes=64, name="to_quantise")
 
-        def spread_edge(g):
+        def prepare_edge_term(g):
+            edge_terms[g] = work.tile([P, PACK, TILES_PER_GROUP, P], F32, tag="ring", bufs=3, align_bytes=64, name="edge_term")
             if not in_range(g):
                 return
             q, half = divmod(g, GROUPS_PER_CHUNK)
-            if half == 0:
-                spreads[q] = psum.tile([P, TILES_PER_CHUNK, P], BF16, tag="spread", name="spread")
-            for j in range(TILES_PER_GROUP):
-                i = TILES_PER_GROUP * half + j
-                m = TILES_PER_CHUNK * q + i
-                nc.tensor.matmul(
-                    out=spreads[q][:, i, :],
-                    lhsT=edge_cols[:, m : m + 1].to_broadcast([P, P]),
-                    rhs=ident_bf[:],
-                    start=True,
-                    stop=True,
-                )
-
-        def prepare_edge_term(g):
-            if not in_range(g) or g % GROUPS_PER_CHUNK != GROUPS_PER_CHUNK - 1:
-                return
-            q = g // GROUPS_PER_CHUNK
-            edge_all = work.tile([P, TILES_PER_CHUNK, P], BF16, tag="edge_all", name="edge_all")
-            nc.vector.tensor_copy(out=edge_all[:], in_=spreads[q][:])
-            edge_term = work.tile([P, PACK, TILES_PER_CHUNK, P], F32, tag="edge_term", bufs=3, name="edge_term")
             for t in range(PACK):
                 nc.gpsimd.tensor_scalar(
-                    out=edge_term[:, t, :, :],
-                    in0=edge_all[:],
+                    out=edge_terms[g][:, t, :, :].rearrange("p j c -> p (j c)"),
+                    in0=edge_all[q][:, GROUP_WORDS * half : GROUP_WORDS * (half + 1)],
                     scalar1=w1_edge[:, t : t + 1],
                     scalar2=b1_f32[:, t : t + 1],
                     op0=ALU.mult,
                     op1=ALU.add,
                 )
-            edge_terms[q] = edge_term
 
-        x_grouped = {}
-        x_codes = {}
-        x_scales = {}
+        codes = {}
+        scales = {}
         sums1 = {}
-        h_grouped = {}
-        h_codes = {}
-        h_scales = {}
+        pre_grouped = {}
         sums2 = {}
-
         x_banks = {}
 
         def transpose_x(g):
@@ -218,22 +185,26 @@ def tile_edgenetwork_kernel(
         def copy_out_x(g, pair):
             if not in_range(g):
                 return
-            if pair == 0:
-                x_grouped[g] = new_grouped()
-            copy_out(x_banks[g], x_grouped[g], pair)
+            copy_out(x_banks[g], to_quantise[g - 2][:, 0:GROUP_VALUES], pair)
 
-        def quantise_x(g):
+        def quantise(k):
+            first = 0 if in_range(k + 2) else 1
+            last = 2 if in_range(k - 2) else 1
+            if first >= last:
+                return
+            codes[k] = work.tile([P, 2 * GROUP_WORDS], U32, tag="codes", bufs=3, align_bytes=64, name="codes")
+            scales[k] = work.tile([P, 2 * GROUP_WORDS], U8, tag="scales", bufs=3, align_bytes=64, name="scales")
+            words = slice(GROUP_WORDS * first, GROUP_WORDS * last)
+            nc.vector.quantize_mx(
+                out=codes[k][:, words].bitcast(FP8X4),
+                scales=scales[k][:, words],
+                in_=to_quantise[k][:, GROUP_VALUES * first : GROUP_VALUES * last],
+            )
+
+        def layer1(g, j):
             if not in_range(g):
                 return
-            x_codes[g] = work.tile([P, TILES_PER_GROUP * P], U32, tag="x_codes", align_bytes=64, name="x_codes")
-            x_scales[g] = work.tile([P, TILES_PER_GROUP * P], U8, tag="x_scales", align_bytes=64, name="x_scales")
-            quantise(x_grouped[g][:], x_codes[g][:], x_scales[g][:])
-
-        def layer1(n):
-            if not 0 <= n < N_TILES:
-                return
-            g, j = divmod(n, TILES_PER_GROUP)
-            sums = psum.tile([P, PACK, P], F32, tag="sums1", bufs=SUMS1_BANKS, name="sums1_tile")
+            sums = psum.tile([P, PACK, P], F32, tag="sums1", bufs=TILES_PER_GROUP, name="sums1_tile")
             cols = slice(P * j, P * (j + 1))
             for t in range(PACK):
                 block = slice(P * t, P * (t + 1))
@@ -241,56 +212,46 @@ def tile_edgenetwork_kernel(
                     out=sums[:, t, :],
                     lhsT=w1_codes[:, block].bitcast(FP8X4),
                     lhsT_scale=w1_scales[:, block],
-                    rhs=x_codes[g][:, cols].bitcast(FP8X4),
-                    rhs_scale=x_scales[g][:, cols],
+                    rhs=codes[g - 2][:, cols].bitcast(FP8X4),
+                    rhs_scale=scales[g - 2][:, cols],
                     start=True,
                     stop=True,
                 )
-            sums1[n] = sums
+            sums1[(g, j)] = sums
 
-        pre_grouped = {}
-
-        def hidden(n):
-            if not 0 <= n < N_TILES:
+        def hidden(g, j):
+            if not in_range(g):
                 return
-            g, j = divmod(n, TILES_PER_GROUP)
-            q, i = divmod(n, TILES_PER_CHUNK)
             if j == 0:
                 pre_grouped[g] = work.tile([P, TILES_PER_GROUP, P * PACK], BF16, tag="pre", bufs=3, align_bytes=64, name="pre")
-                h_grouped[g] = work.tile([P, TILES_PER_GROUP, P * PACK], BF16, tag="h", bufs=3, align_bytes=64, name="h")
             nc.vector.tensor_tensor(
                 out=pre_grouped[g][:, j, :].rearrange("p (b i t) -> p b t i", i=RUN, t=PACK),
-                in0=sums1[n][:].rearrange("p t (b i) -> p b t i", i=RUN),
-                in1=edge_terms[q][:, :, i, :].rearrange("p t (b i) -> p b t i", i=RUN),
+                in0=sums1[(g, j)][:].rearrange("p t (b i) -> p b t i", i=RUN),
+                in1=edge_terms[g][:, :, j, :].rearrange("p t (b i) -> p b t i", i=RUN),
                 op=ALU.add,
             )
 
-        def relu(n):
-            if not 0 <= n < N_TILES:
-                return
-            g, j = divmod(n, TILES_PER_GROUP)
-            if j < RELU_ON_VECTOR:
-                nc.vector.tensor_scalar_max(out=h_grouped[g][:, j, :], in0=pre_grouped[g][:, j, :], scalar1=0.0)
-            else:
-                nc.scalar.activation(out=h_grouped[g][:, j, :], in_=pre_grouped[g][:, j, :], func=ACT.Relu)
-
-        def quantise_h(g):
+        def relu(g, on_vector):
             if not in_range(g):
                 return
-            h_codes[g] = work.tile([P, TILES_PER_GROUP * P], U32, tag="h_codes", align_bytes=64, name="h_codes")
-            h_scales[g] = work.tile([P, TILES_PER_GROUP * P], U8, tag="h_scales", align_bytes=64, name="h_scales")
-            quantise(h_grouped[g][:].rearrange("p j w -> p (j w)"), h_codes[g][:], h_scales[g][:])
+            split = P * PACK * RELU_ON_VECTOR
+            pre = pre_grouped[g][:].rearrange("p j w -> p (j w)")
+            h = to_quantise[g + 2][:, GROUP_VALUES : 2 * GROUP_VALUES]
+            if on_vector and split > 0:
+                nc.vector.tensor_scalar_max(out=h[:, 0:split], in0=pre[:, 0:split], scalar1=0.0)
+            if not on_vector and split < GROUP_VALUES:
+                nc.scalar.activation(out=h[:, split:], in_=pre[:, split:], func=ACT.Relu)
 
         def layer2(g):
             if not in_range(g):
                 return
-            sums = psum.tile([P, TILES_PER_GROUP * P], F32, tag="sums2", name="sums2_tile")
+            sums = psum.tile([P, GROUP_WORDS], F32, tag="sums2", name="sums2_tile")
             nc.tensor.matmul_mx(
                 out=sums[:],
                 lhsT=w2_codes[:].bitcast(FP8X4),
                 lhsT_scale=w2_scales[:],
-                rhs=h_codes[g][:].bitcast(FP8X4),
-                rhs_scale=h_scales[g][:],
+                rhs=codes[g + 2][:, GROUP_WORDS : 2 * GROUP_WORDS].bitcast(FP8X4),
+                rhs_scale=scales[g + 2][:, GROUP_WORDS : 2 * GROUP_WORDS],
                 start=True,
                 stop=True,
             )
@@ -302,7 +263,7 @@ def tile_edgenetwork_kernel(
         def tanh(g):
             if not in_range(g):
                 return
-            out_rows[g] = work.tile([P, TILES_PER_GROUP * P], F32, tag="out_rows", name="out_rows")
+            out_rows[g] = work.tile([P, GROUP_WORDS], F32, tag="out_rows", name="out_rows")
             nc.scalar.activation(out=out_rows[g][:], in_=sums2[g][:], func=ACT.Tanh, bias=b2_f32[:, 0:1])
 
         def transpose_out(g):
@@ -322,31 +283,19 @@ def tile_edgenetwork_kernel(
             first = TILES_PER_GROUP * half
             nc.sync.dma_start(out=out_by_chunk[q][:, first : first + TILES_PER_GROUP, :], in_=result[:])
 
-        for g in range(-2 - EDGE_TERM_AHEAD, -2):
-            spread_edge(g + EDGE_TERM_AHEAD)
-            prepare_edge_term(g + EDGE_TERM_AHEAD)
-        for g in range(-2, N_GROUPS + 2):
-            first_tile = TILES_PER_GROUP * g
-            transpose_x(g + 2)
-            spread_edge(g + EDGE_TERM_AHEAD)
-            hidden(first_tile)
-            layer1(first_tile + SUMS1_BANKS)
-            copy_out_x(g + 2, 0)
-            quantise_x(g + 1)
-            hidden(first_tile + 1)
-            layer1(first_tile + 1 + SUMS1_BANKS)
-            relu(first_tile)
-            relu(first_tile + 1)
-            copy_out_x(g + 2, 1)
-            prepare_edge_term(g + EDGE_TERM_AHEAD)
-            transpose_out(g - 2)
-            hidden(first_tile + 2)
-            layer1(first_tile + 2 + SUMS1_BANKS)
-            relu(first_tile + 2)
-            store(g - 2)
-            quantise_h(g - 1)
-            layer2(g - 1)
-            hidden(first_tile + 3)
-            layer1(first_tile + 3 + SUMS1_BANKS)
-            relu(first_tile + 3)
-            tanh(g - 1)
+        for k in range(-3, N_GROUPS + 3):
+            new_to_quantise(k + 1)
+            transpose_x(k + 3)
+            transpose_out(k - 3)
+            relu(k - 1, True)
+            quantise(k)
+            prepare_edge_term(k + 1)
+            layer2(k - 2)
+            relu(k - 1, False)
+            copy_out_x(k + 3, 0)
+            copy_out_x(k + 3, 1)
+            store(k - 3)
+            tanh(k - 2)
+            for j in range(TILES_PER_GROUP):
+                hidden(k, j)
+                layer1(k + 1, j)

@@ -25,7 +25,8 @@ N_CHUNKS = E // (P * TILES_PER_CHUNK)
 N_GROUPS = N_CHUNKS * GROUPS_PER_CHUNK
 CHUNKS_AHEAD = 3
 RUN = 4
-RELU_ON_VECTOR = 1
+RELU_ON_VECTOR = 2
+SCALAR_BLOCKS = 1
 GROUP_VALUES = TILES_PER_GROUP * P * PACK
 GROUP_WORDS = TILES_PER_GROUP * P
 
@@ -151,12 +152,25 @@ def tile_edgenetwork_kernel(
         def new_to_quantise(k):
             to_quantise[k] = work.tile([P, 2 * GROUP_VALUES], BF16, tag="ring", bufs=3, align_bytes=64, name="to_quantise")
 
+        def edge_term_on_scalar(g):
+            if not in_range(g):
+                return
+            q, half = divmod(g, GROUPS_PER_CHUNK)
+            for t in range(SCALAR_BLOCKS):
+                nc.scalar.activation(
+                    out=edge_terms[g][:, t, :, :].rearrange("p j c -> p (j c)"),
+                    in_=edge_all[q][:, GROUP_WORDS * half : GROUP_WORDS * (half + 1)],
+                    func=ACT.Identity,
+                    bias=b1_f32[:, t : t + 1],
+                    scale=w1_edge[:, t : t + 1],
+                )
+
         def prepare_edge_term(g):
             edge_terms[g] = work.tile([P, PACK, TILES_PER_GROUP, P], F32, tag="ring", bufs=3, align_bytes=64, name="edge_term")
             if not in_range(g):
                 return
             q, half = divmod(g, GROUPS_PER_CHUNK)
-            for t in range(PACK):
+            for t in range(SCALAR_BLOCKS, PACK):
                 nc.gpsimd.tensor_scalar(
                     out=edge_terms[g][:, t, :, :].rearrange("p j c -> p (j c)"),
                     in0=edge_all[q][:, GROUP_WORDS * half : GROUP_WORDS * (half + 1)],
@@ -294,6 +308,7 @@ def tile_edgenetwork_kernel(
             relu(k - 1, False)
             copy_out_x(k + 3, 0)
             copy_out_x(k + 3, 1)
+            edge_term_on_scalar(k + 1)
             store(k - 3)
             tanh(k - 2)
             for j in range(TILES_PER_GROUP):

@@ -25,8 +25,7 @@ N_CHUNKS = E // (P * TILES_PER_CHUNK)
 N_GROUPS = N_CHUNKS * GROUPS_PER_CHUNK
 CHUNKS_AHEAD = 3
 RUN = 4
-RELU_ON_VECTOR = 2
-SCALAR_BLOCKS = 1
+RING_SETS = 3
 GROUP_VALUES = TILES_PER_GROUP * P * PACK
 GROUP_WORDS = TILES_PER_GROUP * P
 
@@ -128,12 +127,14 @@ def tile_edgenetwork_kernel(
                 banks.append(xt)
             return banks
 
-        def copy_out(banks, grouped, pair):
+        def copy_out(banks, grouped, pair, on_vector=False):
             grouped_words = grouped.bitcast(F32)
-            nc.scalar.copy(
-                out=grouped_words[:, 512 * pair : 512 * (pair + 1)].rearrange("p (i c u) -> p i c u", i=2, u=2),
-                in_=banks[pair][:].rearrange("p (i u) c -> p i c u", u=2),
-            )
+            out_words = grouped_words[:, 512 * pair : 512 * (pair + 1)].rearrange("p (i c u) -> p i c u", i=2, u=2)
+            in_words = banks[pair][:].rearrange("p (i u) c -> p i c u", u=2)
+            if on_vector:
+                nc.vector.tensor_copy(out=out_words, in_=in_words)
+            else:
+                nc.scalar.copy(out=out_words, in_=in_words)
 
         w1_codes = const.tile([P, PACK * P], U32, align_bytes=64)
         w1_scales = const.tile([P, PACK * P], U8, align_bytes=64)
@@ -146,34 +147,27 @@ def tile_edgenetwork_kernel(
         def in_range(g):
             return 0 <= g < N_GROUPS
 
-        to_quantise = {}
-        edge_terms = {}
+        ring = const.tile([P, RING_SETS * 4 * GROUP_VALUES], BF16, align_bytes=64)
 
-        def new_to_quantise(k):
-            to_quantise[k] = work.tile([P, 2 * GROUP_VALUES], BF16, tag="ring", bufs=3, align_bytes=64, name="to_quantise")
+        def ring_set(q):
+            first = 4 * GROUP_VALUES * (q % RING_SETS)
+            return ring[:, first : first + 4 * GROUP_VALUES]
 
-        def edge_term_on_scalar(g):
-            if not in_range(g):
+        def to_quantise(k):
+            q = (k + 2) // 2 if k >= 0 else 2
+            first = 2 * GROUP_VALUES * (k % 2)
+            return ring_set(q)[:, first : first + 2 * GROUP_VALUES]
+
+        def edge_term(q):
+            return ring_set(q).bitcast(F32).rearrange("p (t i c) -> p t i c", t=PACK, i=TILES_PER_CHUNK)
+
+        def prepare_edge_term(q, blocks):
+            if not 0 <= q < N_CHUNKS:
                 return
-            q, half = divmod(g, GROUPS_PER_CHUNK)
-            for t in range(SCALAR_BLOCKS):
-                nc.scalar.activation(
-                    out=edge_terms[g][:, t, :, :].rearrange("p j c -> p (j c)"),
-                    in_=edge_all[q][:, GROUP_WORDS * half : GROUP_WORDS * (half + 1)],
-                    func=ACT.Identity,
-                    bias=b1_f32[:, t : t + 1],
-                    scale=w1_edge[:, t : t + 1],
-                )
-
-        def prepare_edge_term(g):
-            edge_terms[g] = work.tile([P, PACK, TILES_PER_GROUP, P], F32, tag="ring", bufs=3, align_bytes=64, name="edge_term")
-            if not in_range(g):
-                return
-            q, half = divmod(g, GROUPS_PER_CHUNK)
-            for t in range(SCALAR_BLOCKS, PACK):
+            for t in blocks:
                 nc.gpsimd.tensor_scalar(
-                    out=edge_terms[g][:, t, :, :].rearrange("p j c -> p (j c)"),
-                    in0=edge_all[q][:, GROUP_WORDS * half : GROUP_WORDS * (half + 1)],
+                    out=edge_term(q)[:, t, :, :].rearrange("p i c -> p (i c)"),
+                    in0=edge_all[q][:],
                     scalar1=w1_edge[:, t : t + 1],
                     scalar2=b1_f32[:, t : t + 1],
                     op0=ALU.mult,
@@ -196,10 +190,10 @@ def tile_edgenetwork_kernel(
             x_sb = x_chunks[q]
             x_banks[g] = transpose_rows([x_sb[:, TILES_PER_GROUP * half + j, :] for j in range(TILES_PER_GROUP)])
 
-        def copy_out_x(g, pair):
+        def copy_out_x(g, pair, on_vector):
             if not in_range(g):
                 return
-            copy_out(x_banks[g], to_quantise[g - 2][:, 0:GROUP_VALUES], pair)
+            copy_out(x_banks[g], to_quantise(g - 2)[:, 0:GROUP_VALUES], pair, on_vector)
 
         def quantise(k):
             first = 0 if in_range(k + 2) else 1
@@ -212,7 +206,7 @@ def tile_edgenetwork_kernel(
             nc.vector.quantize_mx(
                 out=codes[k][:, words].bitcast(FP8X4),
                 scales=scales[k][:, words],
-                in_=to_quantise[k][:, GROUP_VALUES * first : GROUP_VALUES * last],
+                in_=to_quantise(k)[:, GROUP_VALUES * first : GROUP_VALUES * last],
             )
 
         def layer1(g, j):
@@ -236,25 +230,24 @@ def tile_edgenetwork_kernel(
         def hidden(g, j):
             if not in_range(g):
                 return
+            q, half = divmod(g, GROUPS_PER_CHUNK)
             if j == 0:
-                pre_grouped[g] = work.tile([P, TILES_PER_GROUP, P * PACK], BF16, tag="pre", bufs=3, align_bytes=64, name="pre")
+                pre_grouped[g] = work.tile([P, PACK, GROUP_WORDS], BF16, tag="pre", bufs=3, align_bytes=64, name="pre")
             nc.vector.tensor_tensor(
-                out=pre_grouped[g][:, j, :].rearrange("p (b i t) -> p b t i", i=RUN, t=PACK),
-                in0=sums1[(g, j)][:].rearrange("p t (b i) -> p b t i", i=RUN),
-                in1=edge_terms[g][:, :, j, :].rearrange("p t (b i) -> p b t i", i=RUN),
+                out=pre_grouped[g][:, :, P * j : P * (j + 1)],
+                in0=sums1[(g, j)][:],
+                in1=edge_term(q)[:, :, TILES_PER_GROUP * half + j, :],
                 op=ALU.add,
             )
 
-        def relu(g, on_vector):
+        def relu(g):
             if not in_range(g):
                 return
-            split = P * PACK * RELU_ON_VECTOR
-            pre = pre_grouped[g][:].rearrange("p j w -> p (j w)")
-            h = to_quantise[g + 2][:, GROUP_VALUES : 2 * GROUP_VALUES]
-            if on_vector and split > 0:
-                nc.vector.tensor_scalar_max(out=h[:, 0:split], in0=pre[:, 0:split], scalar1=0.0)
-            if not on_vector and split < GROUP_VALUES:
-                nc.scalar.activation(out=h[:, split:], in_=pre[:, split:], func=ACT.Relu)
+            nc.scalar.activation(
+                out=to_quantise(g + 2)[:, GROUP_VALUES : 2 * GROUP_VALUES].rearrange("p (b i t) -> p b t i", i=RUN, t=PACK),
+                in_=pre_grouped[g][:].rearrange("p t (b i) -> p b t i", i=RUN),
+                func=ACT.Relu,
+            )
 
         def layer2(g):
             if not in_range(g):
@@ -297,20 +290,20 @@ def tile_edgenetwork_kernel(
             first = TILES_PER_GROUP * half
             nc.sync.dma_start(out=out_by_chunk[q][:, first : first + TILES_PER_GROUP, :], in_=result[:])
 
+        prepare_edge_term(0, range(PACK))
         for k in range(-3, N_GROUPS + 3):
-            new_to_quantise(k + 1)
             transpose_x(k + 3)
             transpose_out(k - 3)
-            relu(k - 1, True)
             quantise(k)
-            prepare_edge_term(k + 1)
+            if k >= 0:
+                prepare_edge_term((k + 2) // 2, (2 * (k % 2), 2 * (k % 2) + 1))
             layer2(k - 2)
-            relu(k - 1, False)
-            copy_out_x(k + 3, 0)
-            copy_out_x(k + 3, 1)
-            edge_term_on_scalar(k + 1)
+            relu(k - 1)
+            copy_out_x(k + 3, 0, False)
             store(k - 3)
             tanh(k - 2)
             for j in range(TILES_PER_GROUP):
                 hidden(k, j)
                 layer1(k + 1, j)
+                if j == 1:
+                    copy_out_x(k + 3, 1, True)

@@ -71,14 +71,16 @@ def tile_edgenetwork_kernel(
         x_chunks = {}
         edge_all = {}
 
-        def load_chunk(q):
+        def load_chunk(q, parts=1):
             edge_all[q] = work.tile([P, P * TILES_PER_CHUNK], BF16, tag="edge_all", bufs=CHUNKS_AHEAD + 2, name="edge_all")
             nc.sync.dma_start(out=edge_all[q][:], in_=edge_by_chunk[q].partition_broadcast(P))
             x_sb = work.tile([P, TILES_PER_CHUNK, NODE], BF16, tag="x", bufs=CHUNKS_AHEAD + 1, name="x_sb")
-            for rows, first_in, first_x, width in node_inputs:
-                nc.sync.dma_start(
-                    out=x_sb[:, :, first_x : first_x + width], in_=rows[q][:, :, first_in : first_in + width]
-                )
+            for part in range(parts):
+                tiles = slice(TILES_PER_CHUNK // parts * part, TILES_PER_CHUNK // parts * (part + 1))
+                for rows, first_in, first_x, width in node_inputs:
+                    nc.sync.dma_start(
+                        out=x_sb[:, tiles, first_x : first_x + width], in_=rows[q][:, tiles, first_in : first_in + width]
+                    )
             x_chunks[q] = x_sb
 
         w1_rows = const.tile([P, PACK, NODE + 1], BF16)
@@ -87,7 +89,7 @@ def tile_edgenetwork_kernel(
         nc.scalar.dma_start(out=b1_bf[:], in_=b1.rearrange("(p t) -> p t", t=PACK))
         b2_bf = const.tile([P, 1], BF16)
         nc.scalar.dma_start(out=b2_bf[:], in_=b2.rearrange("(p o) -> p o", o=1))
-        load_chunk(0)
+        load_chunk(0, parts=GROUPS_PER_CHUNK)
         load_chunk(1)
 
         w2_codes = const.tile([P, OUT * PACK], U8, align_bytes=64)
@@ -161,18 +163,25 @@ def tile_edgenetwork_kernel(
         def edge_term(q):
             return ring_set(q).bitcast(F32).rearrange("p (t i c) -> p t i c", t=PACK, i=TILES_PER_CHUNK)
 
-        def prepare_edge_term(q, blocks):
+        def prepare_edge_term(q, blocks, tiles=slice(0, TILES_PER_CHUNK), on_scalar=False):
             if not 0 <= q < N_CHUNKS:
                 return
             for t in blocks:
-                nc.gpsimd.tensor_scalar(
-                    out=edge_term(q)[:, t, :, :].rearrange("p i c -> p (i c)"),
-                    in0=edge_all[q][:],
-                    scalar1=w1_edge[:, t : t + 1],
-                    scalar2=b1_f32[:, t : t + 1],
-                    op0=ALU.mult,
-                    op1=ALU.add,
-                )
+                term = edge_term(q)[:, t, tiles, :].rearrange("p i c -> p (i c)")
+                edges = edge_all[q][:, P * tiles.start : P * tiles.stop]
+                if on_scalar:
+                    nc.scalar.activation(
+                        out=term, in_=edges, func=ACT.Identity, bias=b1_f32[:, t : t + 1], scale=w1_edge[:, t : t + 1]
+                    )
+                else:
+                    nc.gpsimd.tensor_scalar(
+                        out=term,
+                        in0=edges,
+                        scalar1=w1_edge[:, t : t + 1],
+                        scalar2=b1_f32[:, t : t + 1],
+                        op0=ALU.mult,
+                        op1=ALU.add,
+                    )
 
         codes = {}
         scales = {}
@@ -193,10 +202,10 @@ def tile_edgenetwork_kernel(
         def copy_out_x(g, pair, on_vector):
             if not in_range(g):
                 return
-            copy_out(x_banks[g], to_quantise(g - 2)[:, 0:GROUP_VALUES], pair, on_vector)
+            copy_out(x_banks[g], to_quantise(g - 1)[:, 0:GROUP_VALUES], pair, on_vector)
 
         def quantise(k):
-            first = 0 if in_range(k + 2) else 1
+            first = 0 if in_range(k + 1) else 1
             last = 2 if in_range(k - 2) else 1
             if first >= last:
                 return
@@ -220,8 +229,8 @@ def tile_edgenetwork_kernel(
                     out=sums[:, t, :],
                     lhsT=w1_codes[:, block].bitcast(FP8X4),
                     lhsT_scale=w1_scales[:, block],
-                    rhs=codes[g - 2][:, cols].bitcast(FP8X4),
-                    rhs_scale=scales[g - 2][:, cols],
+                    rhs=codes[g - 1][:, cols].bitcast(FP8X4),
+                    rhs_scale=scales[g - 1][:, cols],
                     start=True,
                     stop=True,
                 )
@@ -240,14 +249,21 @@ def tile_edgenetwork_kernel(
                 op=ALU.add,
             )
 
-        def relu(g):
+        def relu(g, tiles=slice(0, TILES_PER_GROUP), on_vector=False):
             if not in_range(g):
                 return
-            nc.scalar.activation(
-                out=to_quantise(g + 2)[:, GROUP_VALUES : 2 * GROUP_VALUES].rearrange("p (b i t) -> p b t i", i=RUN, t=PACK),
-                in_=pre_grouped[g][:].rearrange("p t (b i) -> p b t i", i=RUN),
-                func=ACT.Relu,
-            )
+            h = to_quantise(g + 2)[:, GROUP_VALUES + P * PACK * tiles.start : GROUP_VALUES + P * PACK * tiles.stop]
+            pre = pre_grouped[g][:, :, P * tiles.start : P * tiles.stop]
+            if on_vector:
+                nc.vector.tensor_scalar_max(
+                    out=h.rearrange("p (c t) -> p c t", t=PACK), in0=pre.rearrange("p t c -> p c t"), scalar1=0.0
+                )
+            else:
+                nc.scalar.activation(
+                    out=h.rearrange("p (b i t) -> p b t i", i=RUN, t=PACK),
+                    in_=pre.rearrange("p t (b i) -> p b t i", i=RUN),
+                    func=ACT.Relu,
+                )
 
         def layer2(g):
             if not in_range(g):
@@ -281,29 +297,51 @@ def tile_edgenetwork_kernel(
                 nc.tensor.transpose(bank[:, j, :], out_rows[g][:, P * j : P * (j + 1)], ident_f32[:])
             out_banks[g] = bank
 
-        def store(g):
+        def store(g, on_vector=False):
             if not in_range(g):
                 return
             q, half = divmod(g, GROUPS_PER_CHUNK)
             result = work.tile([P, TILES_PER_GROUP, OUT], F32, tag="result", bufs=3, name="result")
-            nc.scalar.copy(out=result[:], in_=out_banks[g][:])
+            if on_vector:
+                nc.vector.tensor_copy(out=result[:], in_=out_banks[g][:])
+            else:
+                nc.scalar.copy(out=result[:], in_=out_banks[g][:])
             first = TILES_PER_GROUP * half
             nc.sync.dma_start(out=out_by_chunk[q][:, first : first + TILES_PER_GROUP, :], in_=result[:])
 
-        prepare_edge_term(0, range(PACK))
-        for k in range(-3, N_GROUPS + 3):
-            transpose_x(k + 3)
+        first_group = slice(0, TILES_PER_GROUP)
+        prepare_edge_term(0, (0, 1), first_group, on_scalar=True)
+        prepare_edge_term(0, (2, 3), first_group)
+        prepare_edge_term(0, range(PACK), slice(TILES_PER_GROUP, TILES_PER_CHUNK))
+        for k in range(-2, N_GROUPS):
+            transpose_x(k + 2)
             transpose_out(k - 3)
             quantise(k)
             if k >= 0:
                 prepare_edge_term((k + 2) // 2, (2 * (k % 2), 2 * (k % 2) + 1))
             layer2(k - 2)
             relu(k - 1)
-            copy_out_x(k + 3, 0, False)
+            copy_out_x(k + 2, 0, False)
             store(k - 3)
             tanh(k - 2)
             for j in range(TILES_PER_GROUP):
                 hidden(k, j)
                 layer1(k + 1, j)
                 if j == 1:
-                    copy_out_x(k + 3, 1, True)
+                    copy_out_x(k + 2, 1, True)
+
+        last = N_GROUPS - 1
+        quantise(last + 1)
+        relu(last, slice(0, TILES_PER_GROUP // 2))
+        relu(last, slice(TILES_PER_GROUP // 2, TILES_PER_GROUP), on_vector=True)
+        layer2(last - 1)
+        transpose_out(last - 2)
+        tanh(last - 1)
+        quantise(last + 2)
+        layer2(last)
+        store(last - 2, on_vector=True)
+        transpose_out(last - 1)
+        tanh(last)
+        store(last - 1, on_vector=True)
+        transpose_out(last)
+        store(last)

@@ -59,7 +59,7 @@ def tile_edgenetwork_kernel(
         (by_chunk(src_node_hidden), 0, 2 * F + H, 2 * F),
         (by_chunk(src_node_hidden), 2 * F, 4 * F + H, F),
     )
-    out_by_chunk = by_chunk(out)
+    out_by_group = out.rearrange("(g p r) n -> g p r n", p=P, r=TILES_PER_GROUP)
     edge_by_chunk = edge_feat.rearrange("(q e) -> q e", e=P * TILES_PER_CHUNK)
 
     with ExitStack() as stack:
@@ -293,21 +293,19 @@ def tile_edgenetwork_kernel(
             if not in_range(g):
                 return
             bank = psum.tile([P, TILES_PER_GROUP, OUT], F32, tag="out_bank", name="out_bank")
-            for j in range(TILES_PER_GROUP):
-                nc.tensor.transpose(bank[:, j, :], out_rows[g][:, P * j : P * (j + 1)], ident_f32[:])
+            for r in range(TILES_PER_GROUP):
+                nc.tensor.transpose(bank[:, r, :], out_rows[g][:, r:GROUP_WORDS:TILES_PER_GROUP], ident_f32[:])
             out_banks[g] = bank
 
         def store(g, on_vector=False):
             if not in_range(g):
                 return
-            q, half = divmod(g, GROUPS_PER_CHUNK)
             result = work.tile([P, TILES_PER_GROUP, OUT], F32, tag="result", bufs=3, name="result")
             if on_vector:
                 nc.vector.tensor_copy(out=result[:], in_=out_banks[g][:])
             else:
                 nc.scalar.copy(out=result[:], in_=out_banks[g][:])
-            first = TILES_PER_GROUP * half
-            nc.sync.dma_start(out=out_by_chunk[q][:, first : first + TILES_PER_GROUP, :], in_=result[:])
+            nc.sync.dma_start(out=out_by_group[g], in_=result[:])
 
         first_group = slice(0, TILES_PER_GROUP)
         prepare_edge_term(0, (0, 1), first_group, on_scalar=True)

@@ -26,6 +26,7 @@ N_GROUPS = N_CHUNKS * GROUPS_PER_CHUNK
 CHUNKS_AHEAD = 3
 RUN = 4
 RING_SETS = 3
+VECTOR_RELU_COLUMNS = 96
 GROUP_VALUES = TILES_PER_GROUP * P * PACK
 GROUP_WORDS = TILES_PER_GROUP * P
 
@@ -249,11 +250,11 @@ def tile_edgenetwork_kernel(
                 op=ALU.add,
             )
 
-        def relu(g, tiles=slice(0, TILES_PER_GROUP), on_vector=False):
+        def relu(g, columns, on_vector):
             if not in_range(g):
                 return
-            h = to_quantise(g + 2)[:, GROUP_VALUES + P * PACK * tiles.start : GROUP_VALUES + P * PACK * tiles.stop]
-            pre = pre_grouped[g][:, :, P * tiles.start : P * tiles.stop]
+            h = to_quantise(g + 2)[:, GROUP_VALUES + PACK * columns.start : GROUP_VALUES + PACK * columns.stop]
+            pre = pre_grouped[g][:, :, columns]
             if on_vector:
                 nc.vector.tensor_scalar_max(
                     out=h.rearrange("p (c t) -> p c t", t=PACK), in0=pre.rearrange("p t c -> p c t"), scalar1=0.0
@@ -315,23 +316,23 @@ def tile_edgenetwork_kernel(
             transpose_x(k + 2)
             transpose_out(k - 3)
             quantise(k)
+            relu(k - 1, slice(0, VECTOR_RELU_COLUMNS), True)
             if k >= 0:
                 prepare_edge_term((k + 2) // 2, (2 * (k % 2), 2 * (k % 2) + 1))
             layer2(k - 2)
-            relu(k - 1)
+            relu(k - 1, slice(VECTOR_RELU_COLUMNS, GROUP_WORDS), False)
             copy_out_x(k + 2, 0, False)
+            copy_out_x(k + 2, 1, False)
             store(k - 3)
             tanh(k - 2)
             for j in range(TILES_PER_GROUP):
                 hidden(k, j)
                 layer1(k + 1, j)
-                if j == 1:
-                    copy_out_x(k + 2, 1, True)
 
         last = N_GROUPS - 1
         quantise(last + 1)
-        relu(last, slice(0, TILES_PER_GROUP // 2))
-        relu(last, slice(TILES_PER_GROUP // 2, TILES_PER_GROUP), on_vector=True)
+        relu(last, slice(0, GROUP_WORDS // 2), False)
+        relu(last, slice(GROUP_WORDS // 2, GROUP_WORDS), True)
         layer2(last - 1)
         transpose_out(last - 2)
         tanh(last - 1)

@@ -26,7 +26,8 @@ N_GROUPS = N_CHUNKS * GROUPS_PER_CHUNK
 CHUNKS_AHEAD = 3
 RUN = 4
 RING_SETS = 3
-VECTOR_RELU_COLUMNS = 96
+VECTOR_RELU_COLUMNS = 160
+SCALAR_TERM_TILES = 2
 GROUP_VALUES = TILES_PER_GROUP * P * PACK
 GROUP_WORDS = TILES_PER_GROUP * P
 
@@ -317,10 +318,14 @@ def tile_edgenetwork_kernel(
             transpose_out(k - 3)
             quantise(k)
             relu(k - 1, slice(0, VECTOR_RELU_COLUMNS), True)
+            split = TILES_PER_CHUNK - SCALAR_TERM_TILES
             if k >= 0:
-                prepare_edge_term((k + 2) // 2, (2 * (k % 2), 2 * (k % 2) + 1))
+                prepare_edge_term((k + 2) // 2, (2 * (k % 2),))
+                prepare_edge_term((k + 2) // 2, (2 * (k % 2) + 1,), slice(0, split))
             layer2(k - 2)
             relu(k - 1, slice(VECTOR_RELU_COLUMNS, GROUP_WORDS), False)
+            if k >= 0:
+                prepare_edge_term((k + 2) // 2, (2 * (k % 2) + 1,), slice(split, TILES_PER_CHUNK), on_scalar=True)
             copy_out_x(k + 2, 0, False)
             copy_out_x(k + 2, 1, False)
             store(k - 3)

@@ -220,34 +220,33 @@ def tile_edgenetwork_kernel(
                 in_=to_quantise(k)[:, GROUP_VALUES * first : GROUP_VALUES * last],
             )
 
-        def layer1(g, j):
+        def layer1(g, t):
             if not in_range(g):
                 return
-            sums = psum.tile([P, PACK, P], F32, tag="sums1", bufs=TILES_PER_GROUP, name="sums1_tile")
-            cols = slice(P * j, P * (j + 1))
-            for t in range(PACK):
-                block = slice(P * t, P * (t + 1))
-                nc.tensor.matmul_mx(
-                    out=sums[:, t, :],
-                    lhsT=w1_codes[:, block].bitcast(FP8X4),
-                    lhsT_scale=w1_scales[:, block],
-                    rhs=codes[g - 1][:, cols].bitcast(FP8X4),
-                    rhs_scale=scales[g - 1][:, cols],
-                    start=True,
-                    stop=True,
-                )
-            sums1[(g, j)] = sums
+            sums = psum.tile([P, GROUP_WORDS], F32, tag="sums1", bufs=PACK, name="sums1_tile")
+            block = slice(P * t, P * (t + 1))
+            nc.tensor.matmul_mx(
+                out=sums[:],
+                lhsT=w1_codes[:, block].bitcast(FP8X4),
+                lhsT_scale=w1_scales[:, block],
+                rhs=codes[g - 1][:, 0:GROUP_WORDS].bitcast(FP8X4),
+                rhs_scale=scales[g - 1][:, 0:GROUP_WORDS],
+                start=True,
+                stop=True,
+            )
+            sums1[(g, t)] = sums
 
-        def hidden(g, j):
+        def hidden(g, t):
             if not in_range(g):
                 return
             q, half = divmod(g, GROUPS_PER_CHUNK)
-            if j == 0:
+            if t == 0:
                 pre_grouped[g] = work.tile([P, PACK, GROUP_WORDS], BF16, tag="pre", bufs=3, align_bytes=64, name="pre")
+            tiles = slice(TILES_PER_GROUP * half, TILES_PER_GROUP * (half + 1))
             nc.vector.tensor_tensor(
-                out=pre_grouped[g][:, :, P * j : P * (j + 1)],
-                in0=sums1[(g, j)][:],
-                in1=edge_term(q)[:, :, TILES_PER_GROUP * half + j, :],
+                out=pre_grouped[g][:, t, :],
+                in0=sums1[(g, t)][:],
+                in1=edge_term(q)[:, t, tiles, :].rearrange("p i c -> p (i c)"),
                 op=ALU.add,
             )
 
@@ -330,9 +329,9 @@ def tile_edgenetwork_kernel(
             copy_out_x(k + 2, 1, False)
             store(k - 3)
             tanh(k - 2)
-            for j in range(TILES_PER_GROUP):
-                hidden(k, j)
-                layer1(k + 1, j)
+            for t in range(PACK):
+                hidden(k, t)
+                layer1(k + 1, t)
 
         last = N_GROUPS - 1
         quantise(last + 1)

@@ -27,7 +27,7 @@ CHUNKS_AHEAD = 3
 RUN = 4
 RING_SETS = 3
 VECTOR_RELU_COLUMNS = 160
-SCALAR_TERM_TILES = 2
+SCALAR_TERM_TILES = 1
 GROUP_VALUES = TILES_PER_GROUP * P * PACK
 GROUP_WORDS = TILES_PER_GROUP * P
 
@@ -54,14 +54,14 @@ def tile_edgenetwork_kernel(
         return rows.rearrange("(q i c) f -> q c i f", c=P, i=TILES_PER_CHUNK)
 
     node_inputs = (
-        (by_chunk(dst_node_feat), 0, 0, F),
-        (by_chunk(dst_node_hidden), 0, F, 2 * F),
-        (by_chunk(dst_node_hidden), 2 * F, 3 * F, F),
-        (by_chunk(src_node_feat), 0, F + H, F),
-        (by_chunk(src_node_hidden), 0, 2 * F + H, 2 * F),
-        (by_chunk(src_node_hidden), 2 * F, 4 * F + H, F),
+        (by_chunk(dst_node_hidden), 0, 0, 2 * F),
+        (by_chunk(dst_node_hidden), 2 * F, 2 * F, F),
+        (by_chunk(dst_node_feat), 0, H, F),
+        (by_chunk(src_node_hidden), 0, F + H, 2 * F),
+        (by_chunk(src_node_hidden), 2 * F, 3 * F + H, F),
+        (by_chunk(src_node_feat), 0, F + 2 * H, F),
     )
-    out_by_group = out.rearrange("(g p r) n -> g p r n", p=P, r=TILES_PER_GROUP)
+    w1_columns = ((F, 0, H), (0, H, F), (2 * F + H, F + H, H), (F + H, F + 2 * H, F))
     edge_by_chunk = edge_feat.rearrange("(q e) -> q e", e=P * TILES_PER_CHUNK)
 
     with ExitStack() as stack:
@@ -75,14 +75,15 @@ def tile_edgenetwork_kernel(
 
         def load_chunk(q, parts=1):
             edge_all[q] = work.tile([P, P * TILES_PER_CHUNK], BF16, tag="edge_all", bufs=CHUNKS_AHEAD + 2, name="edge_all")
-            nc.sync.dma_start(out=edge_all[q][:], in_=edge_by_chunk[q].partition_broadcast(P))
-            x_sb = work.tile([P, TILES_PER_CHUNK, NODE], BF16, tag="x", bufs=CHUNKS_AHEAD + 1, name="x_sb")
+            x_sb = work.tile([P, TILES_PER_CHUNK, NODE], BF16, tag="x", bufs=CHUNKS_AHEAD + 1, align_bytes=1024, name="x_sb")
             for part in range(parts):
                 tiles = slice(TILES_PER_CHUNK // parts * part, TILES_PER_CHUNK // parts * (part + 1))
                 for rows, first_in, first_x, width in node_inputs:
                     nc.sync.dma_start(
                         out=x_sb[:, tiles, first_x : first_x + width], in_=rows[q][:, tiles, first_in : first_in + width]
                     )
+                if part == 0:
+                    nc.sync.dma_start(out=edge_all[q][:], in_=edge_by_chunk[q].partition_broadcast(P))
             x_chunks[q] = x_sb
 
         w1_rows = const.tile([P, PACK, NODE + 1], BF16)
@@ -92,7 +93,7 @@ def tile_edgenetwork_kernel(
         b2_bf = const.tile([P, 1], BF16)
         nc.scalar.dma_start(out=b2_bf[:], in_=b2.rearrange("(p o) -> p o", o=1))
         load_chunk(0, parts=GROUPS_PER_CHUNK)
-        load_chunk(1)
+        load_chunk(1, parts=GROUPS_PER_CHUNK)
 
         w2_codes = const.tile([P, OUT * PACK], U8, align_bytes=64)
         nc.sync.dma_start(
@@ -106,13 +107,16 @@ def tile_edgenetwork_kernel(
                 out=w2_scales[32 * quadrant : 32 * quadrant + 4, :].bitcast(I32),
                 in_=W2_scales[0, 4 * quadrant : 4 * quadrant + 4, :].bitcast(I32),
             )
-        load_chunk(2)
+        load_chunk(2, parts=GROUPS_PER_CHUNK)
 
         ident_f32 = const.tile([P, P], F32)
         make_identity(nc, ident_f32[:])
 
         w1_nodes = const.tile([P, PACK, NODE], BF16)
-        nc.vector.tensor_copy(out=w1_nodes[:], in_=w1_rows[:, :, 0:NODE])
+        for first_in, first_x, width in w1_columns:
+            nc.vector.tensor_copy(
+                out=w1_nodes[:, :, first_x : first_x + width], in_=w1_rows[:, :, first_in : first_in + width]
+            )
         w1_edge = const.tile([P, PACK], F32)
         nc.vector.tensor_copy(out=w1_edge[:], in_=w1_rows[:, :, NODE])
         b1_f32 = const.tile([P, PACK], F32)
@@ -140,12 +144,22 @@ def tile_edgenetwork_kernel(
             else:
                 nc.scalar.copy(out=out_words, in_=in_words)
 
+        zeros = const.tile([P, GROUP_WORDS], BF16)
+        nc.gpsimd.memset(zeros[:], 0.0)
+
+        def keep_warm(passes):
+            unread = psum.tile([P, GROUP_WORDS], F32, tag="sums1", bufs=PACK, name="unread")
+            for n in range(passes):
+                nc.tensor.matmul(unread[:], zeros[:, 0:P], zeros[:], start=True, stop=True)
+
+        keep_warm(6)
+
         w1_codes = const.tile([P, PACK * P], U32, align_bytes=64)
         w1_scales = const.tile([P, PACK * P], U8, align_bytes=64)
         w1_banks = transpose_rows([w1_nodes[:, t, :] for t in range(PACK)])
         w1_grouped = const.tile([P, GROUP_VALUES], BF16, align_bytes=64)
         copy_out(w1_banks, w1_grouped[:], 0)
-        copy_out(w1_banks, w1_grouped[:], 1)
+        copy_out(w1_banks, w1_grouped[:], 1, on_vector=True)
         nc.vector.quantize_mx(out=w1_codes[:].bitcast(FP8X4), scales=w1_scales[:], in_=w1_grouped[:])
 
         def in_range(g):
@@ -163,13 +177,13 @@ def tile_edgenetwork_kernel(
             return ring_set(q)[:, first : first + 2 * GROUP_VALUES]
 
         def edge_term(q):
-            return ring_set(q).bitcast(F32).rearrange("p (t i c) -> p t i c", t=PACK, i=TILES_PER_CHUNK)
+            return ring_set(q).bitcast(F32).rearrange("p (t e) -> p t e", t=PACK)
 
         def prepare_edge_term(q, blocks, tiles=slice(0, TILES_PER_CHUNK), on_scalar=False):
             if not 0 <= q < N_CHUNKS:
                 return
             for t in blocks:
-                term = edge_term(q)[:, t, tiles, :].rearrange("p i c -> p (i c)")
+                term = edge_term(q)[:, t, P * tiles.start : P * tiles.stop]
                 edges = edge_all[q][:, P * tiles.start : P * tiles.stop]
                 if on_scalar:
                     nc.scalar.activation(
@@ -220,6 +234,17 @@ def tile_edgenetwork_kernel(
                 in_=to_quantise(k)[:, GROUP_VALUES * first : GROUP_VALUES * last],
             )
 
+        def quantise_hidden(g, columns):
+            if g + 2 not in codes:
+                codes[g + 2] = work.tile([P, 2 * GROUP_WORDS], U32, tag="codes", bufs=3, align_bytes=64, name="codes")
+                scales[g + 2] = work.tile([P, 2 * GROUP_WORDS], U8, tag="scales", bufs=3, align_bytes=64, name="scales")
+            words = slice(GROUP_WORDS + columns.start, GROUP_WORDS + columns.stop)
+            nc.vector.quantize_mx(
+                out=codes[g + 2][:, words].bitcast(FP8X4),
+                scales=scales[g + 2][:, words],
+                in_=to_quantise(g + 2)[:, PACK * words.start : PACK * words.stop],
+            )
+
         def layer1(g, t):
             if not in_range(g):
                 return
@@ -236,17 +261,19 @@ def tile_edgenetwork_kernel(
             )
             sums1[(g, t)] = sums
 
-        def hidden(g, t):
+        every_column = slice(0, GROUP_WORDS)
+
+        def hidden(g, t, columns=every_column):
             if not in_range(g):
                 return
             q, half = divmod(g, GROUPS_PER_CHUNK)
-            if t == 0:
+            if g not in pre_grouped:
                 pre_grouped[g] = work.tile([P, PACK, GROUP_WORDS], BF16, tag="pre", bufs=3, align_bytes=64, name="pre")
-            tiles = slice(TILES_PER_GROUP * half, TILES_PER_GROUP * (half + 1))
+            first = GROUP_WORDS * half
             nc.vector.tensor_tensor(
-                out=pre_grouped[g][:, t, :],
-                in0=sums1[(g, t)][:],
-                in1=edge_term(q)[:, t, tiles, :].rearrange("p i c -> p (i c)"),
+                out=pre_grouped[g][:, t, columns],
+                in0=sums1[(g, t)][:, columns],
+                in1=edge_term(q)[:, t, first + columns.start : first + columns.stop],
                 op=ALU.add,
             )
 
@@ -266,85 +293,129 @@ def tile_edgenetwork_kernel(
                     func=ACT.Relu,
                 )
 
-        def layer2(g):
+        def layer2(g, columns=every_column, tag="sums2"):
             if not in_range(g):
                 return
-            sums = psum.tile([P, GROUP_WORDS], F32, tag="sums2", name="sums2_tile")
+            bufs = 1 if tag == "sums2" else 2
+            sums = psum.tile([P, columns.stop - columns.start], F32, tag=tag, bufs=bufs, name="sums2_tile")
+            words = slice(GROUP_WORDS + columns.start, GROUP_WORDS + columns.stop)
             nc.tensor.matmul_mx(
                 out=sums[:],
                 lhsT=w2_codes[:].bitcast(FP8X4),
                 lhsT_scale=w2_scales[:],
-                rhs=codes[g + 2][:, GROUP_WORDS : 2 * GROUP_WORDS].bitcast(FP8X4),
-                rhs_scale=scales[g + 2][:, GROUP_WORDS : 2 * GROUP_WORDS],
+                rhs=codes[g + 2][:, words].bitcast(FP8X4),
+                rhs_scale=scales[g + 2][:, words],
                 start=True,
                 stop=True,
             )
-            sums2[g] = sums
+            sums2[(g, columns.start)] = sums
 
         out_rows = {}
         out_banks = {}
 
-        def tanh(g):
+        def tanh(g, columns=every_column):
             if not in_range(g):
                 return
-            out_rows[g] = work.tile([P, GROUP_WORDS], F32, tag="out_rows", name="out_rows")
-            nc.scalar.activation(out=out_rows[g][:], in_=sums2[g][:], func=ACT.Tanh, bias=b2_f32[:, 0:1])
+            rows = work.tile([P, columns.stop - columns.start], F32, tag="out_rows", bufs=3, name="out_rows")
+            nc.scalar.activation(out=rows[:], in_=sums2[(g, columns.start)][:], func=ACT.Tanh, bias=b2_f32[:, 0:1])
+            out_rows[(g, columns.start)] = rows
 
-        def transpose_out(g):
+        def transpose_out(g, columns=every_column, tag="out_bank"):
             if not in_range(g):
                 return
-            bank = psum.tile([P, TILES_PER_GROUP, OUT], F32, tag="out_bank", name="out_bank")
-            for r in range(TILES_PER_GROUP):
-                nc.tensor.transpose(bank[:, r, :], out_rows[g][:, r:GROUP_WORDS:TILES_PER_GROUP], ident_f32[:])
-            out_banks[g] = bank
+            bufs = 1 if tag == "out_bank" else 2
+            width = columns.stop - columns.start
+            each = width // P
+            bank = psum.tile([P, each, OUT], F32, tag=tag, bufs=bufs, name="out_bank")
+            for r in range(each):
+                nc.tensor.transpose(bank[:, r, :], out_rows[(g, columns.start)][:, r:width:each], ident_f32[:])
+            out_banks[(g, columns.start)] = bank
 
-        def store(g, on_vector=False):
+        def store(g, columns=every_column, on_vector=False):
             if not in_range(g):
                 return
-            result = work.tile([P, TILES_PER_GROUP, OUT], F32, tag="result", bufs=3, name="result")
+            each = (columns.stop - columns.start) // P
+            result = work.tile([P, each, OUT], F32, tag="result", bufs=5, name="result")
             if on_vector:
-                nc.vector.tensor_copy(out=result[:], in_=out_banks[g][:])
+                nc.vector.tensor_copy(out=result[:], in_=out_banks[(g, columns.start)][:])
             else:
-                nc.scalar.copy(out=result[:], in_=out_banks[g][:])
-            nc.sync.dma_start(out=out_by_group[g], in_=result[:])
+                nc.scalar.copy(out=result[:], in_=out_banks[(g, columns.start)][:])
+            first = GROUP_WORDS * g
+            rows = out[first + columns.start : first + columns.stop, :].rearrange("(p r) n -> p r n", r=each)
+            nc.sync.dma_start(out=rows, in_=result[:])
 
         first_group = slice(0, TILES_PER_GROUP)
+        keep_warm(4)
+        transpose_x(0)
+        keep_warm(2)
+        copy_out_x(0, 0, False)
+        copy_out_x(0, 1, True)
+        quantise(-1)
         prepare_edge_term(0, (0, 1), first_group, on_scalar=True)
         prepare_edge_term(0, (2, 3), first_group)
         prepare_edge_term(0, range(PACK), slice(TILES_PER_GROUP, TILES_PER_CHUNK))
-        for k in range(-2, N_GROUPS):
+        transpose_x(1)
+        keep_warm(2)
+        for t in range(PACK):
+            layer1(0, t)
+        copy_out_x(1, 0, False)
+        copy_out_x(1, 1, False)
+        hidden(0, 0)
+        hidden(0, 1)
+
+        split = TILES_PER_CHUNK - SCALAR_TERM_TILES
+        vector_columns = slice(0, VECTOR_RELU_COLUMNS)
+        scalar_columns = slice(VECTOR_RELU_COLUMNS, GROUP_WORDS)
+        last = N_GROUPS - 1
+        for k in range(last):
             transpose_x(k + 2)
             transpose_out(k - 3)
             quantise(k)
-            relu(k - 1, slice(0, VECTOR_RELU_COLUMNS), True)
-            split = TILES_PER_CHUNK - SCALAR_TERM_TILES
-            if k >= 0:
-                prepare_edge_term((k + 2) // 2, (2 * (k % 2),))
-                prepare_edge_term((k + 2) // 2, (2 * (k % 2) + 1,), slice(0, split))
+            relu(k - 1, vector_columns, True)
+            prepare_edge_term((k + 2) // 2, (2 * (k % 2),))
+            prepare_edge_term((k + 2) // 2, (2 * (k % 2) + 1,), slice(0, split))
             layer2(k - 2)
-            relu(k - 1, slice(VECTOR_RELU_COLUMNS, GROUP_WORDS), False)
-            if k >= 0:
-                prepare_edge_term((k + 2) // 2, (2 * (k % 2) + 1,), slice(split, TILES_PER_CHUNK), on_scalar=True)
+            relu(k - 1, scalar_columns, False)
+            prepare_edge_term((k + 2) // 2, (2 * (k % 2) + 1,), slice(split, TILES_PER_CHUNK), on_scalar=True)
             copy_out_x(k + 2, 0, False)
             copy_out_x(k + 2, 1, False)
             store(k - 3)
             tanh(k - 2)
             for t in range(PACK):
-                hidden(k, t)
+                if (k, t) not in ((0, 0), (0, 1)):
+                    hidden(k, t)
                 layer1(k + 1, t)
 
-        last = N_GROUPS - 1
+        halves = (slice(0, GROUP_WORDS // 2), slice(GROUP_WORDS // 2, GROUP_WORDS))
+        three_quarters = 3 * GROUP_WORDS // 4
+        transpose_out(last - 3)
+        quantise(last)
+        relu(last - 1, vector_columns, True)
+        layer2(last - 2)
+        relu(last - 1, scalar_columns, False)
+        store(last - 3)
+        tanh(last - 2)
+        for t in range(PACK):
+            hidden(last, t, halves[0])
         quantise(last + 1)
-        relu(last, slice(0, GROUP_WORDS // 2), False)
-        relu(last, slice(GROUP_WORDS // 2, GROUP_WORDS), True)
-        layer2(last - 1)
+        relu(last, halves[0], False)
         transpose_out(last - 2)
+        layer2(last - 1)
+        for t in range(PACK):
+            hidden(last, t, halves[1])
         tanh(last - 1)
-        quantise(last + 2)
-        layer2(last)
+        quantise_hidden(last, halves[0])
+        relu(last, slice(halves[1].start, three_quarters), False)
+        relu(last, slice(three_quarters, GROUP_WORDS), True)
+        layer2(last, halves[0], tag="xt")
+        transpose_out(last - 1, tag="xt")
+        quantise_hidden(last, halves[1])
+        layer2(last, halves[1])
+        tanh(last, halves[0])
         store(last - 2, on_vector=True)
-        transpose_out(last - 1)
-        tanh(last)
         store(last - 1, on_vector=True)
-        transpose_out(last)
-        store(last)
+        transpose_out(last, halves[0])
+        tanh(last, halves[1])
+        store(last, halves[0], on_vector=True)
+        transpose_out(last, halves[1], tag="xt")
+        store(last, halves[1])

@@ -92,8 +92,8 @@ def tile_edgenetwork_kernel(
         nc.scalar.dma_start(out=b1_bf[:], in_=b1.rearrange("(p t) -> p t", t=PACK))
         b2_bf = const.tile([P, 1], BF16)
         nc.scalar.dma_start(out=b2_bf[:], in_=b2.rearrange("(p o) -> p o", o=1))
-        load_chunk(0, parts=GROUPS_PER_CHUNK)
-        load_chunk(1, parts=GROUPS_PER_CHUNK)
+        load_chunk(0)
+        load_chunk(1)
 
         w2_codes = const.tile([P, OUT * PACK], U8, align_bytes=64)
         nc.sync.dma_start(
@@ -107,7 +107,7 @@ def tile_edgenetwork_kernel(
                 out=w2_scales[32 * quadrant : 32 * quadrant + 4, :].bitcast(I32),
                 in_=W2_scales[0, 4 * quadrant : 4 * quadrant + 4, :].bitcast(I32),
             )
-        load_chunk(2, parts=GROUPS_PER_CHUNK)
+        load_chunk(2)
 
         ident_f32 = const.tile([P, P], F32)
         make_identity(nc, ident_f32[:])
@@ -147,12 +147,12 @@ def tile_edgenetwork_kernel(
         zeros = const.tile([P, GROUP_WORDS], BF16)
         nc.gpsimd.memset(zeros[:], 0.0)
 
-        def keep_warm(passes):
+        def keep_warm(moving_operands):
             unread = psum.tile([P, GROUP_WORDS], F32, tag="sums1", bufs=PACK, name="unread")
-            for n in range(passes):
-                nc.tensor.matmul(unread[:], zeros[:, 0:P], zeros[:], start=True, stop=True)
+            for moving in moving_operands:
+                nc.tensor.matmul(unread[:, 0 : moving.shape[1]], zeros[:, 0:P], moving, start=True, stop=True)
 
-        keep_warm(6)
+        keep_warm([zeros[:]] * 6)
 
         w1_codes = const.tile([P, PACK * P], U32, align_bytes=64)
         w1_scales = const.tile([P, PACK * P], U8, align_bytes=64)
@@ -211,7 +211,7 @@ def tile_edgenetwork_kernel(
                 return
             q, half = divmod(g, GROUPS_PER_CHUNK)
             if half == 0 and q + CHUNKS_AHEAD < N_CHUNKS:
-                load_chunk(q + CHUNKS_AHEAD)
+                load_chunk(q + CHUNKS_AHEAD, parts=GROUPS_PER_CHUNK if q + CHUNKS_AHEAD == N_CHUNKS - 1 else 1)
             x_sb = x_chunks[q]
             x_banks[g] = transpose_rows([x_sb[:, TILES_PER_GROUP * half + j, :] for j in range(TILES_PER_GROUP)])
 
@@ -345,9 +345,9 @@ def tile_edgenetwork_kernel(
             nc.sync.dma_start(out=rows, in_=result[:])
 
         first_group = slice(0, TILES_PER_GROUP)
-        keep_warm(4)
+        keep_warm([x_chunks[0][:, i, F + H : 3 * F + H] for i in range(TILES_PER_CHUNK)])
+        keep_warm([x_chunks[0][:, i, 3 * F + H : 4 * F + H] for i in range(TILES_PER_CHUNK)])
         transpose_x(0)
-        keep_warm(2)
         copy_out_x(0, 0, False)
         copy_out_x(0, 1, True)
         quantise(-1)
@@ -355,7 +355,6 @@ def tile_edgenetwork_kernel(
         prepare_edge_term(0, (2, 3), first_group)
         prepare_edge_term(0, range(PACK), slice(TILES_PER_GROUP, TILES_PER_CHUNK))
         transpose_x(1)
-        keep_warm(2)
         for t in range(PACK):
             layer1(0, t)
         copy_out_x(1, 0, False)

@@ -94,6 +94,7 @@ def tile_edgenetwork_kernel(
         nc.scalar.dma_start(out=b2_bf[:], in_=b2.rearrange("(p o) -> p o", o=1))
         load_chunk(0)
         load_chunk(1)
+        load_chunk(2)
 
         w2_codes = const.tile([P, OUT * PACK], U8, align_bytes=64)
         nc.sync.dma_start(
@@ -107,7 +108,6 @@ def tile_edgenetwork_kernel(
                 out=w2_scales[32 * quadrant : 32 * quadrant + 4, :].bitcast(I32),
                 in_=W2_scales[0, 4 * quadrant : 4 * quadrant + 4, :].bitcast(I32),
             )
-        load_chunk(2)
 
         ident_f32 = const.tile([P, P], F32)
         make_identity(nc, ident_f32[:])
@@ -362,31 +362,44 @@ def tile_edgenetwork_kernel(
         hidden(0, 0)
         hidden(0, 1)
 
-        split = TILES_PER_CHUNK - SCALAR_TERM_TILES
         vector_columns = slice(0, VECTOR_RELU_COLUMNS)
         scalar_columns = slice(VECTOR_RELU_COLUMNS, GROUP_WORDS)
         last = N_GROUPS - 1
         for k in range(last):
-            transpose_x(k + 2)
+            ahead_of_load = k == 0
+            behind_load = k == 1
+            if not ahead_of_load:
+                transpose_x(k + 2)
             transpose_out(k - 3)
+            if behind_load:
+                for t in range(PACK):
+                    hidden(k, t)
             quantise(k)
             relu(k - 1, vector_columns, True)
+            split = TILES_PER_CHUNK - SCALAR_TERM_TILES if k >= GROUPS_PER_CHUNK else TILES_PER_CHUNK
             prepare_edge_term((k + 2) // 2, (2 * (k % 2),))
             prepare_edge_term((k + 2) // 2, (2 * (k % 2) + 1,), slice(0, split))
             layer2(k - 2)
-            relu(k - 1, scalar_columns, False)
-            prepare_edge_term((k + 2) // 2, (2 * (k % 2) + 1,), slice(split, TILES_PER_CHUNK), on_scalar=True)
+            if not behind_load:
+                relu(k - 1, scalar_columns, False)
+            if split < TILES_PER_CHUNK:
+                prepare_edge_term((k + 2) // 2, (2 * (k % 2) + 1,), slice(split, TILES_PER_CHUNK), on_scalar=True)
+            for t in range(PACK):
+                if not behind_load and (k, t) not in ((0, 0), (0, 1)):
+                    hidden(k, t)
+                layer1(k + 1, t)
+            if ahead_of_load:
+                tanh(k - 2)
+                relu(k, scalar_columns, False)
+                transpose_x(k + 2)
             copy_out_x(k + 2, 0, False)
             copy_out_x(k + 2, 1, False)
             store(k - 3)
-            tanh(k - 2)
-            for t in range(PACK):
-                if (k, t) not in ((0, 0), (0, 1)):
-                    hidden(k, t)
-                layer1(k + 1, t)
+            if not ahead_of_load:
+                tanh(k - 2)
 
         halves = (slice(0, GROUP_WORDS // 2), slice(GROUP_WORDS // 2, GROUP_WORDS))
-        three_quarters = 3 * GROUP_WORDS // 4
+        scalar_end = halves[1].start + P // 2
         transpose_out(last - 3)
         quantise(last)
         relu(last - 1, vector_columns, True)
@@ -398,14 +411,14 @@ def tile_edgenetwork_kernel(
             hidden(last, t, halves[0])
         quantise(last + 1)
         relu(last, halves[0], False)
-        transpose_out(last - 2)
         layer2(last - 1)
+        transpose_out(last - 2)
         for t in range(PACK):
             hidden(last, t, halves[1])
+        relu(last, slice(halves[1].start, scalar_end), False)
         tanh(last - 1)
         quantise_hidden(last, halves[0])
-        relu(last, slice(halves[1].start, three_quarters), False)
-        relu(last, slice(three_quarters, GROUP_WORDS), True)
+        relu(last, slice(scalar_end, GROUP_WORDS), True)
         layer2(last, halves[0], tag="xt")
         transpose_out(last - 1, tag="xt")
         quantise_hidden(last, halves[1])
@@ -413,8 +426,8 @@ def tile_edgenetwork_kernel(
         tanh(last, halves[0])
         store(last - 2, on_vector=True)
         store(last - 1, on_vector=True)
-        transpose_out(last, halves[0])
         tanh(last, halves[1])
+        transpose_out(last, halves[0])
         store(last, halves[0], on_vector=True)
         transpose_out(last, halves[1], tag="xt")
         store(last, halves[1])

from contextlib import ExitStack

import concourse.mybir as mybir
from concourse.masks import make_identity

F32 = mybir.dt.float32
BF16 = mybir.dt.bfloat16
U32 = mybir.dt.uint32
U8 = mybir.dt.uint8
I32 = mybir.dt.int32
FP8X4 = mybir.dt.float8_e4m3fn_x4
ALU = mybir.AluOpType
ACT = mybir.ActivationFunctionType

P = 128
PACK = 4
E, F, H, MID, OUT = 16384, 64, 192, 512, 128
NODE = 2 * (F + H)
NODE_WORDS = NODE // 2

TILES_PER_GROUP = 4
TILES_PER_CHUNK = 8
GROUPS_PER_CHUNK = TILES_PER_CHUNK // TILES_PER_GROUP
N_CHUNKS = E // (P * TILES_PER_CHUNK)
N_GROUPS = N_CHUNKS * GROUPS_PER_CHUNK
CHUNKS_AHEAD = 3
RUN = 4
RING_SETS = 3
VECTOR_RELU_COLUMNS = 160
SCALAR_TERM_TILES = 1
GROUP_VALUES = TILES_PER_GROUP * P * PACK
GROUP_WORDS = TILES_PER_GROUP * P

FLOPS = 2 * E * ((NODE + 1) * MID + MID * OUT)


def tile_edgenetwork_kernel(
    tc,
    dst_node_feat,
    dst_node_hidden,
    src_node_feat,
    src_node_hidden,
    edge_feat,
    W1,
    b1,
    W2_words,
    W2_scales,
    b2,
    out,
):
    nc = tc.nc

    def by_chunk(rows):
        return rows.rearrange("(q i c) f -> q c i f", c=P, i=TILES_PER_CHUNK)

    node_inputs = (
        (by_chunk(dst_node_hidden), 0, 0, 2 * F),
        (by_chunk(dst_node_hidden), 2 * F, 2 * F, F),
        (by_chunk(dst_node_feat), 0, H, F),
        (by_chunk(src_node_hidden), 0, F + H, 2 * F),
        (by_chunk(src_node_hidden), 2 * F, 3 * F + H, F),
        (by_chunk(src_node_feat), 0, F + 2 * H, F),
    )
    w1_columns = ((F, 0, H), (0, H, F), (2 * F + H, F + H, H), (F + H, F + 2 * H, F))
    edge_by_chunk = edge_feat.rearrange("(q e) -> q e", e=P * TILES_PER_CHUNK)

    with ExitStack() as stack:
        const = stack.enter_context(tc.tile_pool(name="const", bufs=1))
        work = stack.enter_context(tc.tile_pool(name="work", bufs=2))
        psum = stack.enter_context(tc.psum_pool(name="psum", bufs=1))
        stack.enter_context(tc.manual_schedule())

        x_chunks = {}
        edge_all = {}

        def load_chunk(q, parts=1):
            edge_all[q] = work.tile([P, P * TILES_PER_CHUNK], BF16, tag="edge_all", bufs=CHUNKS_AHEAD + 2, name="edge_all")
            x_sb = work.tile([P, TILES_PER_CHUNK, NODE], BF16, tag="x", bufs=CHUNKS_AHEAD + 1, align_bytes=1024, name="x_sb")
            for part in range(parts):
                tiles = slice(TILES_PER_CHUNK // parts * part, TILES_PER_CHUNK // parts * (part + 1))
                for rows, first_in, first_x, width in node_inputs:
                    nc.sync.dma_start(
                        out=x_sb[:, tiles, first_x : first_x + width], in_=rows[q][:, tiles, first_in : first_in + width]
                    )
                if part == 0:
                    nc.sync.dma_start(out=edge_all[q][:], in_=edge_by_chunk[q].partition_broadcast(P))
            x_chunks[q] = x_sb

        w1_rows = const.tile([P, PACK, NODE + 1], BF16)
        nc.sync.dma_start(out=w1_rows[:], in_=W1.rearrange("(j t) k -> j t k", t=PACK))
        b1_bf = const.tile([P, PACK], BF16)
        nc.scalar.dma_start(out=b1_bf[:], in_=b1.rearrange("(p t) -> p t", t=PACK))
        b2_bf = const.tile([P, 1], BF16)
        nc.scalar.dma_start(out=b2_bf[:], in_=b2.rearrange("(p o) -> p o", o=1))
        load_chunk(0)
        load_chunk(1)
        load_chunk(2)

        w2_codes = const.tile([P, OUT * PACK], U8, align_bytes=64)
        nc.sync.dma_start(
            out=w2_codes[:].bitcast(I32),
            in_=W2_words.rearrange("g p n t -> (g p) (n t)").bitcast(I32),
        )
        w2_scales = const.tile([P, OUT], U8, align_bytes=64)
        nc.vector.memset(w2_scales[:].bitcast(I32), 0)
        for quadrant in range(4):
            nc.sync.dma_start(
                out=w2_scales[32 * quadrant : 32 * quadrant + 4, :].bitcast(I32),
                in_=W2_scales[0, 4 * quadrant : 4 * quadrant + 4, :].bitcast(I32),
            )

        ident_f32 = const.tile([P, P], F32)
        make_identity(nc, ident_f32[:])

        w1_nodes = const.tile([P, PACK, NODE], BF16)
        for first_in, first_x, width in w1_columns:
            nc.vector.tensor_copy(
                out=w1_nodes[:, :, first_x : first_x + width], in_=w1_rows[:, :, first_in : first_in + width]
            )
        w1_edge = const.tile([P, PACK], F32)
        nc.vector.tensor_copy(out=w1_edge[:], in_=w1_rows[:, :, NODE])
        b1_f32 = const.tile([P, PACK], F32)
        nc.vector.tensor_copy(out=b1_f32[:], in_=b1_bf[:])
        b2_f32 = const.tile([P, 1], F32)
        nc.vector.tensor_copy(out=b2_f32[:], in_=b2_bf[:])

        def transpose_rows(row_tiles):
            banks = []
            for pair in range(2):
                xt = psum.tile([P, 4, P], F32, tag="xt", bufs=2, name="xt")
                for i in range(2):
                    words = row_tiles[2 * pair + i].bitcast(F32)
                    for u in range(2):
                        nc.tensor.transpose(xt[:, 2 * i + u, :], words[:, u:NODE_WORDS:2], ident_f32[:])
                banks.append(xt)
            return banks

        def copy_out(banks, grouped, pair, on_vector=False):
            grouped_words = grouped.bitcast(F32)
            out_words = grouped_words[:, 512 * pair : 512 * (pair + 1)].rearrange("p (i c u) -> p i c u", i=2, u=2)
            in_words = banks[pair][:].rearrange("p (i u) c -> p i c u", u=2)
            if on_vector:
                nc.vector.tensor_copy(out=out_words, in_=in_words)
            else:
                nc.scalar.copy(out=out_words, in_=in_words)

        zeros = const.tile([P, GROUP_WORDS], BF16)
        nc.gpsimd.memset(zeros[:], 0.0)

        def keep_warm(moving_operands):
            unread = psum.tile([P, GROUP_WORDS], F32, tag="sums1", bufs=PACK, name="unread")
            for moving in moving_operands:
                nc.tensor.matmul(unread[:, 0 : moving.shape[1]], zeros[:, 0:P], moving, start=True, stop=True)

        keep_warm([zeros[:]] * 6)

        w1_codes = const.tile([P, PACK * P], U32, align_bytes=64)
        w1_scales = const.tile([P, PACK * P], U8, align_bytes=64)
        w1_banks = transpose_rows([w1_nodes[:, t, :] for t in range(PACK)])
        w1_grouped = const.tile([P, GROUP_VALUES], BF16, align_bytes=64)
        copy_out(w1_banks, w1_grouped[:], 0)
        copy_out(w1_banks, w1_grouped[:], 1, on_vector=True)
        nc.vector.quantize_mx(out=w1_codes[:].bitcast(FP8X4), scales=w1_scales[:], in_=w1_grouped[:])

        def in_range(g):
            return 0 <= g < N_GROUPS

        ring = const.tile([P, RING_SETS * 4 * GROUP_VALUES], BF16, align_bytes=64)

        def ring_set(q):
            first = 4 * GROUP_VALUES * (q % RING_SETS)
            return ring[:, first : first + 4 * GROUP_VALUES]

        def to_quantise(k):
            q = (k + 2) // 2 if k >= 0 else 2
            first = 2 * GROUP_VALUES * (k % 2)
            return ring_set(q)[:, first : first + 2 * GROUP_VALUES]

        def edge_term(q):
            return ring_set(q).bitcast(F32).rearrange("p (t e) -> p t e", t=PACK)

        def prepare_edge_term(q, blocks, tiles=slice(0, TILES_PER_CHUNK), on_scalar=False):
            if not 0 <= q < N_CHUNKS:
                return
            for t in blocks:
                term = edge_term(q)[:, t, P * tiles.start : P * tiles.stop]
                edges = edge_all[q][:, P * tiles.start : P * tiles.stop]
                if on_scalar:
                    nc.scalar.activation(
                        out=term, in_=edges, func=ACT.Identity, bias=b1_f32[:, t : t + 1], scale=w1_edge[:, t : t + 1]
                    )
                else:
                    nc.gpsimd.tensor_scalar(
                        out=term,
                        in0=edges,
                        scalar1=w1_edge[:, t : t + 1],
                        scalar2=b1_f32[:, t : t + 1],
                        op0=ALU.mult,
                        op1=ALU.add,
                    )

        codes = {}
        scales = {}
        sums1 = {}
        pre_grouped = {}
        sums2 = {}
        x_banks = {}

        def transpose_x(g):
            if not in_range(g):
                return
            q, half = divmod(g, GROUPS_PER_CHUNK)
            if half == 0 and q + CHUNKS_AHEAD < N_CHUNKS:
                load_chunk(q + CHUNKS_AHEAD, parts=GROUPS_PER_CHUNK if q + CHUNKS_AHEAD == N_CHUNKS - 1 else 1)
            x_sb = x_chunks[q]
            x_banks[g] = transpose_rows([x_sb[:, TILES_PER_GROUP * half + j, :] for j in range(TILES_PER_GROUP)])

        def copy_out_x(g, pair, on_vector):
            if not in_range(g):
                return
            copy_out(x_banks[g], to_quantise(g - 1)[:, 0:GROUP_VALUES], pair, on_vector)

        def quantise(k):
            first = 0 if in_range(k + 1) else 1
            last = 2 if in_range(k - 2) else 1
            if first >= last:
                return
            codes[k] = work.tile([P, 2 * GROUP_WORDS], U32, tag="codes", bufs=3, align_bytes=64, name="codes")
            scales[k] = work.tile([P, 2 * GROUP_WORDS], U8, tag="scales", bufs=3, align_bytes=64, name="scales")
            words = slice(GROUP_WORDS * first, GROUP_WORDS * last)
            nc.vector.quantize_mx(
                out=codes[k][:, words].bitcast(FP8X4),
                scales=scales[k][:, words],
                in_=to_quantise(k)[:, GROUP_VALUES * first : GROUP_VALUES * last],
            )

        def quantise_hidden(g, columns):
            if g + 2 not in codes:
                codes[g + 2] = work.tile([P, 2 * GROUP_WORDS], U32, tag="codes", bufs=3, align_bytes=64, name="codes")
                scales[g + 2] = work.tile([P, 2 * GROUP_WORDS], U8, tag="scales", bufs=3, align_bytes=64, name="scales")
            words = slice(GROUP_WORDS + columns.start, GROUP_WORDS + columns.stop)
            nc.vector.quantize_mx(
                out=codes[g + 2][:, words].bitcast(FP8X4),
                scales=scales[g + 2][:, words],
                in_=to_quantise(g + 2)[:, PACK * words.start : PACK * words.stop],
            )

        def layer1(g, t):
            if not in_range(g):
                return
            sums = psum.tile([P, GROUP_WORDS], F32, tag="sums1", bufs=PACK, name="sums1_tile")
            block = slice(P * t, P * (t + 1))
            nc.tensor.matmul_mx(
                out=sums[:],
                lhsT=w1_codes[:, block].bitcast(FP8X4),
                lhsT_scale=w1_scales[:, block],
                rhs=codes[g - 1][:, 0:GROUP_WORDS].bitcast(FP8X4),
                rhs_scale=scales[g - 1][:, 0:GROUP_WORDS],
                start=True,
                stop=True,
            )
            sums1[(g, t)] = sums

        every_column = slice(0, GROUP_WORDS)

        def hidden(g, t, columns=every_column):
            if not in_range(g):
                return
            q, half = divmod(g, GROUPS_PER_CHUNK)
            if g not in pre_grouped:
                pre_grouped[g] = work.tile([P, PACK, GROUP_WORDS], BF16, tag="pre", bufs=3, align_bytes=64, name="pre")
            first = GROUP_WORDS * half
            nc.vector.tensor_tensor(
                out=pre_grouped[g][:, t, columns],
                in0=sums1[(g, t)][:, columns],
                in1=edge_term(q)[:, t, first + columns.start : first + columns.stop],
                op=ALU.add,
            )

        def relu(g, columns, on_vector):
            if not in_range(g):
                return
            h = to_quantise(g + 2)[:, GROUP_VALUES + PACK * columns.start : GROUP_VALUES + PACK * columns.stop]
            pre = pre_grouped[g][:, :, columns]
            if on_vector:
                nc.vector.tensor_scalar_max(
                    out=h.rearrange("p (c t) -> p c t", t=PACK), in0=pre.rearrange("p t c -> p c t"), scalar1=0.0
                )
            else:
                nc.scalar.activation(
                    out=h.rearrange("p (b i t) -> p b t i", i=RUN, t=PACK),
                    in_=pre.rearrange("p t (b i) -> p b t i", i=RUN),
                    func=ACT.Relu,
                )

        def layer2(g, columns=every_column, tag="sums2"):
            if not in_range(g):
                return
            bufs = 1 if tag == "sums2" else 2
            sums = psum.tile([P, columns.stop - columns.start], F32, tag=tag, bufs=bufs, name="sums2_tile")
            words = slice(GROUP_WORDS + columns.start, GROUP_WORDS + columns.stop)
            nc.tensor.matmul_mx(
                out=sums[:],
                lhsT=w2_codes[:].bitcast(FP8X4),
                lhsT_scale=w2_scales[:],
                rhs=codes[g + 2][:, words].bitcast(FP8X4),
                rhs_scale=scales[g + 2][:, words],
                start=True,
                stop=True,
            )
            sums2[(g, columns.start)] = sums

        out_rows = {}
        out_banks = {}

        def tanh(g, columns=every_column):
            if not in_range(g):
                return
            rows = work.tile([P, columns.stop - columns.start], F32, tag="out_rows", bufs=3, name="out_rows")
            nc.scalar.activation(out=rows[:], in_=sums2[(g, columns.start)][:], func=ACT.Tanh, bias=b2_f32[:, 0:1])
            out_rows[(g, columns.start)] = rows

        def transpose_out(g, columns=every_column, tag="out_bank"):
            if not in_range(g):
                return
            bufs = 1 if tag == "out_bank" else 2
            width = columns.stop - columns.start
            each = width // P
            bank = psum.tile([P, each, OUT], F32, tag=tag, bufs=bufs, name="out_bank")
            for r in range(each):
                nc.tensor.transpose(bank[:, r, :], out_rows[(g, columns.start)][:, r:width:each], ident_f32[:])
            out_banks[(g, columns.start)] = bank

        def store(g, columns=every_column, on_vector=False):
            if not in_range(g):
                return
            each = (columns.stop - columns.start) // P
            result = work.tile([P, each, OUT], F32, tag="result", bufs=5, name="result")
            if on_vector:
                nc.vector.tensor_copy(out=result[:], in_=out_banks[(g, columns.start)][:])
            else:
                nc.scalar.copy(out=result[:], in_=out_banks[(g, columns.start)][:])
            first = GROUP_WORDS * g
            rows = out[first + columns.start : first + columns.stop, :].rearrange("(p r) n -> p r n", r=each)
            nc.sync.dma_start(out=rows, in_=result[:])

        first_group = slice(0, TILES_PER_GROUP)
        keep_warm([x_chunks[0][:, i, F + H : 3 * F + H] for i in range(TILES_PER_CHUNK)])
        keep_warm([x_chunks[0][:, i, 3 * F + H : 4 * F + H] for i in range(TILES_PER_CHUNK)])
        transpose_x(0)
        copy_out_x(0, 0, False)
        copy_out_x(0, 1, True)
        quantise(-1)
        prepare_edge_term(0, (0, 1), first_group, on_scalar=True)
        prepare_edge_term(0, (2, 3), first_group)
        prepare_edge_term(0, range(PACK), slice(TILES_PER_GROUP, TILES_PER_CHUNK))
        transpose_x(1)
        for t in range(PACK):
            layer1(0, t)
        copy_out_x(1, 0, False)
        copy_out_x(1, 1, False)
        hidden(0, 0)
        hidden(0, 1)

        vector_columns = slice(0, VECTOR_RELU_COLUMNS)
        scalar_columns = slice(VECTOR_RELU_COLUMNS, GROUP_WORDS)
        last = N_GROUPS - 1
        for k in range(last):
            ahead_of_load = k == 0
            behind_load = k == 1
            if not ahead_of_load:
                transpose_x(k + 2)
            transpose_out(k - 3)
            if behind_load:
                for t in range(PACK):
                    hidden(k, t)
            quantise(k)
            relu(k - 1, vector_columns, True)
            split = TILES_PER_CHUNK - SCALAR_TERM_TILES if k >= GROUPS_PER_CHUNK else TILES_PER_CHUNK
            prepare_edge_term((k + 2) // 2, (2 * (k % 2),))
            prepare_edge_term((k + 2) // 2, (2 * (k % 2) + 1,), slice(0, split))
            layer2(k - 2)
            if not behind_load:
                relu(k - 1, scalar_columns, False)
            if split < TILES_PER_CHUNK:
                prepare_edge_term((k + 2) // 2, (2 * (k % 2) + 1,), slice(split, TILES_PER_CHUNK), on_scalar=True)
            for t in range(PACK):
                if not behind_load and (k, t) not in ((0, 0), (0, 1)):
                    hidden(k, t)
                layer1(k + 1, t)
            if ahead_of_load:
                tanh(k - 2)
                relu(k, scalar_columns, False)
                transpose_x(k + 2)
            copy_out_x(k + 2, 0, False)
            copy_out_x(k + 2, 1, False)
            store(k - 3)
            if not ahead_of_load:
                tanh(k - 2)

        halves = (slice(0, GROUP_WORDS // 2), slice(GROUP_WORDS // 2, GROUP_WORDS))
        scalar_end = halves[1].start + P // 2
        transpose_out(last - 3)
        quantise(last)
        relu(last - 1, vector_columns, True)
        layer2(last - 2)
        relu(last - 1, scalar_columns, False)
        store(last - 3)
        tanh(last - 2)
        for t in range(PACK):
            hidden(last, t, halves[0])
        quantise(last + 1)
        relu(last, halves[0], False)
        layer2(last - 1)
        transpose_out(last - 2)
        for t in range(PACK):
            hidden(last, t, halves[1])
        relu(last, slice(halves[1].start, scalar_end), False)
        tanh(last - 1)
        quantise_hidden(last, halves[0])
        relu(last, slice(scalar_end, GROUP_WORDS), True)
        layer2(last, halves[0], tag="xt")
        transpose_out(last - 1, tag="xt")
        quantise_hidden(last, halves[1])
        layer2(last, halves[1])
        tanh(last, halves[0])
        store(last - 2, on_vector=True)
        store(last - 1, on_vector=True)
        tanh(last, halves[1])
        transpose_out(last, halves[0])
        store(last, halves[0], on_vector=True)
        transpose_out(last, halves[1], tag="xt")
        store(last, halves[1])
